import numpy as np
import ml_dtypes


def mxq(x, axis, fmt="e4m3"):
    dtype, down = {"e4m3": (ml_dtypes.float8_e4m3fn, 7), "e5m2": (ml_dtypes.float8_e5m2, 14)}[fmt]
    v = np.moveaxis(np.asarray(x, np.float32).astype(ml_dtypes.bfloat16).astype(np.float64), axis, -1)
    blocks = v.reshape(v.shape[:-1] + (-1, 32))
    amax = np.abs(blocks).max(-1, keepdims=True)
    byte = np.maximum(np.where(amax > 0, np.frexp(amax)[1] - 1 + 127, 0) - down, 1)
    scale = np.exp2(byte - 127.0)
    codes = (blocks / scale).astype(np.float32).astype(dtype).astype(np.float64)
    return np.moveaxis((codes * scale).reshape(v.shape), -1, axis)


WIDE = False


def mx_kscale(k):
    if not WIDE:
        return np.ones(k)
    levels = np.array([10, -10, 5, -5, 0])
    a = np.random.permutation(np.resize(levels, k // 512 * 4)).reshape(k // 512, 4)
    idx = np.arange(k)
    return np.exp2(a[idx // 512, idx % 128 // 32])


BF16 = ml_dtypes.bfloat16


def bf(x):
    return np.asarray(x, np.float32).astype(BF16)


def f64(x):
    return np.asarray(x).astype(np.float64)


N, M, D = 1024, 8192, 512


def setup_inputs():
    a = 0.7 / D ** 0.25
    s = mx_kscale(D)
    t = np.maximum(s, 1.0 / s) ** 2
    X = np.random.standard_normal((N, D)) * a
    SV = np.random.standard_normal((M, D)) * a
    SV[: M // 16] *= t[None, :]
    return {"X": bf(X),
            "SV": bf(SV),
            "DC": bf(np.random.standard_normal((1, M)) * 8.0 / np.sqrt(M)),
            "IC": bf(np.random.standard_normal(1)),
            "gamma": bf((2.0 + 0.1 * np.random.standard_normal(1)) / np.sqrt(D))}


def reference(X, SV, DC, IC, gamma):
    X, SV = f64(X), f64(SV)
    x2 = np.sum(X * X, axis=1)
    sv2 = np.sum(SV * SV, axis=1)
    cross = mxq(X, 1, "e4m3") @ mxq(SV, 1, "e4m3").T
    d2 = np.maximum(x2[:, None] + sv2[None, :] - 2.0 * cross, 0.0)
    k = np.exp(-f64(gamma) * d2)
    return np.sum(k * f64(DC), axis=1) + f64(IC)

@@ -1,0 +1,183 @@
+from contextlib import ExitStack
+
+import concourse.mybir as mybir
+from concourse.masks import make_identity
+
+F32 = mybir.dt.float32
+BF16 = mybir.dt.bfloat16
+U32 = mybir.dt.uint32
+U8 = mybir.dt.uint8
+FP8X4 = mybir.dt.float8_e4m3fn_x4
+ALU = mybir.AluOpType
+ACT = mybir.ActivationFunctionType
+AX = mybir.AxisListType
+
+P = 128
+N_ROWS = 1024
+M_ROWS = 8192
+D = 512
+WORDS = D // 2
+NB = N_ROWS // P
+MB_COLS = 512
+N_MB = M_ROWS // MB_COLS
+TILES_PER_MB = MB_COLS // P
+GROUPS = [[0], [1], [2, 3], [4, 5, 6, 7], [8, 9, 10, 11], [12, 13, 14, 15]]
+
+FLOPS = 2 * N_ROWS * M_ROWS * D
+
+
+def tile_rbf_svm_kernel(tc, X, SV, DC, IC, gamma, out):
+    nc = tc.nc
+    n_groups = len(GROUPS)
+    with ExitStack() as ctx:
+        const = ctx.enter_context(tc.tile_pool(name="const", bufs=1))
+        keep = ctx.enter_context(tc.tile_pool(name="keep", bufs=1))
+        svload = ctx.enter_context(tc.tile_pool(name="svload", bufs=4))
+        stage = ctx.enter_context(tc.tile_pool(name="stage", bufs=3))
+        work = ctx.enter_context(tc.tile_pool(name="work", bufs=4))
+        junkp = ctx.enter_context(tc.tile_pool(name="junkp", bufs=2))
+        ps_mm = ctx.enter_context(tc.psum_pool(name="ps_mm", bufs=4))
+        ps_t = ctx.enter_context(tc.psum_pool(name="ps_t", bufs=2))
+        ps_b = ctx.enter_context(tc.psum_pool(name="ps_b", bufs=2))
+
+        x_nat = keep.tile([P, NB * D], BF16)
+        nc.sync.dma_start(
+            out=x_nat[:].rearrange("p (j d) -> p j d", j=NB),
+            in_=X.rearrange("(p j) d -> p j d", j=NB),
+        )
+        g_bf = const.tile([P, 1], BF16)
+        nc.scalar.dma_start(out=g_bf[:], in_=gamma.partition_broadcast(P))
+        ic_bf = const.tile([P, 1], BF16)
+        nc.scalar.dma_start(out=ic_bf[:], in_=IC.partition_broadcast(P))
+
+        sv_nat = {}
+
+        def load_sv(mb):
+            t = svload.tile([P, TILES_PER_MB * D], BF16, name="sv_nat")
+            nc.sync.dma_start(
+                out=t[:].rearrange("p (j d) -> p j d", j=TILES_PER_MB),
+                in_=SV[mb * MB_COLS:(mb + 1) * MB_COLS, :].rearrange("(j p) d -> p j d", p=P),
+            )
+            sv_nat[mb] = t
+
+        load_sv(0)
+        load_sv(1)
+        dcb = keep.tile([P, M_ROWS], BF16)
+        nc.scalar.dma_start(out=dcb[:], in_=DC.rearrange("o m -> (o m)").partition_broadcast(P))
+
+        warm = const.tile([P, 1], F32)
+        nc.vector.memset(warm[:], 0.0)
+        nc.scalar.activation(out=warm[:], in_=warm[:], func=ACT.Exp)
+        ident = const.tile([P, P], F32)
+        make_identity(nc, ident[:])
+        half_ident = const.tile([P, P], F32)
+        nc.vector.tensor_scalar(out=half_ident[:], in0=ident[:], scalar1=0.5, scalar2=None, op0=ALU.mult)
+        g2 = const.tile([P, 1], F32)
+        nc.vector.tensor_scalar(out=g2[:], in0=g_bf[:], scalar1=2.0, scalar2=None, op0=ALU.mult)
+        ic_f = const.tile([P, 1], F32)
+        nc.vector.tensor_copy(out=ic_f[:], in_=ic_bf[:])
+
+        x2col = keep.tile([P, NB], F32)
+        hx2 = keep.tile([P, NB], F32)
+        sv2col = keep.tile([P, M_ROWS // P], F32)
+        hsv2b = keep.tile([P, M_ROWS], F32)
+        acc = keep.tile([P, NB * n_groups], F32)
+
+        xq = keep.tile([P, N_ROWS], U32, align_bytes=64)
+        xs = keep.tile([P, N_ROWS], U8, align_bytes=64)
+        svq = keep.tile([P, M_ROWS], U32, align_bytes=64)
+        svs = keep.tile([P, M_ROWS], U8, align_bytes=64)
+
+        def transpose_group(src_f32, n_tiles, grouped_f32, on_vector):
+            for pair in range(n_tiles // 2):
+                xt = ps_t.tile([P, 4, P], F32, name="xt")
+                for jj in range(2):
+                    for u in range(2):
+                        c0 = (2 * pair + jj) * WORDS + u * P
+                        nc.tensor.transpose(xt[:, 2 * jj + u, :], src_f32[:, c0:c0 + P], ident[:])
+                dst = grouped_f32[:, pair * 512:(pair + 1) * 512].rearrange(
+                    "p (j r u) -> p j r u", j=2, u=2)
+                src = xt[:].rearrange("p (j u) r -> p j r u", j=2)
+                if on_vector:
+                    nc.vector.tensor_copy(out=dst, in_=src)
+                else:
+                    nc.scalar.copy(out=dst, in_=src)
+
+        def square_sum(src, col):
+            junk = junkp.tile([P, D], BF16, name="junk")
+            nc.scalar.activation(out=junk[:], in_=src, func=ACT.Square, accum_out=col)
+
+        gx = keep.tile([P, N_ROWS * 4], BF16, align_bytes=64)
+        transpose_group(x_nat[:].bitcast(F32), NB, gx[:].bitcast(F32), True)
+        nc.vector.quantize_mx(out=xq[:].bitcast(FP8X4), scales=xs[:], in_=gx[:])
+
+        def prep_x_norm(j):
+            square_sum(x_nat[:, j * D:(j + 1) * D], x2col[:, j:j + 1])
+            nc.vector.tensor_scalar(out=hx2[:, j:j + 1], in0=x2col[:, j:j + 1], scalar1=0.5,
+                                    scalar2=None, op0=ALU.mult)
+
+        def prep_sv(mb, on_vector):
+            t = sv_nat[mb]
+            cols = slice(mb * MB_COLS, (mb + 1) * MB_COLS)
+            for j in range(TILES_PER_MB):
+                c = mb * TILES_PER_MB + j
+                square_sum(t[:, j * D:(j + 1) * D], sv2col[:, c:c + 1])
+            grouped = stage.tile([P, MB_COLS * 4], BF16, align_bytes=64, name="grouped")
+            transpose_group(t[:].bitcast(F32), TILES_PER_MB, grouped[:].bitcast(F32), on_vector)
+            nc.vector.quantize_mx(out=svq[:, cols].bitcast(FP8X4), scales=svs[:, cols], in_=grouped[:])
+            bc = ps_b.tile([P, MB_COLS], F32, name="bc")
+            for j in range(TILES_PER_MB):
+                c = mb * TILES_PER_MB + j
+                nc.tensor.matmul(out=bc[:, j * P:(j + 1) * P],
+                                 lhsT=sv2col[:, c:c + 1].to_broadcast([P, P]),
+                                 rhs=half_ident[:], start=True, stop=True)
+            nc.scalar.copy(out=hsv2b[:, cols], in_=bc[:])
+            if mb + 2 < N_MB:
+                load_sv(mb + 2)
+
+        def main_step(g, nb):
+            mbs = GROUPS[g]
+            width = len(mbs) * MB_COLS
+            w = work.tile([P, 4 * MB_COLS], F32, name="w")
+            for i, mb in enumerate(mbs):
+                cols = slice(mb * MB_COLS, (mb + 1) * MB_COLS)
+                ps = ps_mm.tile([P, MB_COLS], F32, name="ps")
+                nc.tensor.matmul_mx(
+                    out=ps[:],
+                    lhsT=xq[:, nb * P:(nb + 1) * P].bitcast(FP8X4),
+                    lhsT_scale=xs[:, nb * P:(nb + 1) * P],
+                    rhs=svq[:, cols].bitcast(FP8X4),
+                    rhs_scale=svs[:, cols],
+                    start=True, stop=True,
+                )
+                nc.vector.scalar_tensor_tensor(
+                    out=w[:, i * MB_COLS:(i + 1) * MB_COLS], in0=ps[:], scalar=hx2[:, nb:nb + 1],
+                    in1=hsv2b[:, cols], op0=ALU.subtract, op1=ALU.subtract)
+            nc.scalar.activation(out=w[:, :width], in_=w[:, :width], func=ACT.Exp, scale=g2[:, 0:1])
+            c0 = mbs[0] * MB_COLS
+            k = nb * n_groups + g
+            nc.vector.scalar_tensor_tensor(
+                out=w[:, :width], in0=w[:, :width], scalar=1.0, in1=dcb[:, c0:c0 + width],
+                op0=ALU.min, op1=ALU.mult, accum_out=acc[:, k:k + 1])
+
+        prep_x_norm(0)
+        prep_sv(0, True)
+        for j in range(1, NB):
+            prep_x_norm(j)
+
+        for g in range(n_groups):
+            nxt = GROUPS[g + 1] if g + 1 < n_groups else []
+            when = {}
+            for i, mb in enumerate(nxt):
+                when[(i * NB) // len(nxt)] = when.get((i * NB) // len(nxt), []) + [mb]
+            for nb in range(NB):
+                for mb in when.get(nb, []):
+                    prep_sv(mb, False)
+                main_step(g, nb)
+
+        res = const.tile([P, NB], F32)
+        nc.vector.tensor_reduce(out=res[:], in_=acc[:].rearrange("p (j g) -> p j g", g=n_groups),
+                                axis=AX.X, op=ALU.add)
+        res2 = const.tile([P, NB], F32)
+        nc.vector.tensor_scalar(out=res2[:], in0=res[:], scalar1=ic_f[:, 0:1], scalar2=None, op0=ALU.add)
+        nc.sync.dma_start(out=out.rearrange("(p j) -> p j", j=NB), in_=res2[:])

@@ -18,27 +18,30 @@ M_ROWS = 8192
 D = 512
 WORDS = D // 2
 NB = N_ROWS // P
+HALF = 512
 MB_COLS = 512
 N_MB = M_ROWS // MB_COLS
 TILES_PER_MB = MB_COLS // P
-GROUPS = [[0], [1], [2, 3], [4, 5, 6, 7], [8, 9, 10, 11], [12, 13, 14, 15]]
+N_SVT = M_ROWS // P
+SVT_PER_W = 2
+N_W = N_SVT // SVT_PER_W
+LAG = 2
 
 FLOPS = 2 * N_ROWS * M_ROWS * D
 
 
 def tile_rbf_svm_kernel(tc, X, SV, DC, IC, gamma, out):
     nc = tc.nc
-    n_groups = len(GROUPS)
     with ExitStack() as ctx:
         const = ctx.enter_context(tc.tile_pool(name="const", bufs=1))
         keep = ctx.enter_context(tc.tile_pool(name="keep", bufs=1))
         svload = ctx.enter_context(tc.tile_pool(name="svload", bufs=4))
         stage = ctx.enter_context(tc.tile_pool(name="stage", bufs=3))
-        work = ctx.enter_context(tc.tile_pool(name="work", bufs=4))
+        work = ctx.enter_context(tc.tile_pool(name="work", bufs=6))
         junkp = ctx.enter_context(tc.tile_pool(name="junkp", bufs=2))
         ps_mm = ctx.enter_context(tc.psum_pool(name="ps_mm", bufs=4))
-        ps_t = ctx.enter_context(tc.psum_pool(name="ps_t", bufs=2))
-        ps_b = ctx.enter_context(tc.psum_pool(name="ps_b", bufs=2))
+        ps_t = ctx.enter_context(tc.psum_pool(name="ps_t", bufs=3))
+        ps_r = ctx.enter_context(tc.psum_pool(name="ps_r", bufs=1))
 
         x_nat = keep.tile([P, NB * D], BF16)
         nc.sync.dma_start(
@@ -49,6 +52,9 @@ def tile_rbf_svm_kernel(tc, X, SV, DC, IC, gamma, out):
         nc.scalar.dma_start(out=g_bf[:], in_=gamma.partition_broadcast(P))
         ic_bf = const.tile([P, 1], BF16)
         nc.scalar.dma_start(out=ic_bf[:], in_=IC.partition_broadcast(P))
+        dc_rows = const.tile([P, P], BF16)
+        nc.vector.memset(dc_rows[:], 0.0)
+        nc.scalar.dma_start(out=dc_rows[0:N_SVT, :], in_=DC.rearrange("o (t p) -> (o t) p", p=P))
 
         sv_nat = {}
 
@@ -62,14 +68,15 @@ def tile_rbf_svm_kernel(tc, X, SV, DC, IC, gamma, out):
 
         load_sv(0)
         load_sv(1)
-        dcb = keep.tile([P, M_ROWS], BF16)
-        nc.scalar.dma_start(out=dcb[:], in_=DC.rearrange("o m -> (o m)").partition_broadcast(P))
+        load_sv(2)
 
         warm = const.tile([P, 1], F32)
         nc.vector.memset(warm[:], 0.0)
         nc.scalar.activation(out=warm[:], in_=warm[:], func=ACT.Exp)
         ident = const.tile([P, P], F32)
         make_identity(nc, ident[:])
+        ident_bf = const.tile([P, P], BF16)
+        nc.vector.tensor_copy(out=ident_bf[:], in_=ident[:])
         half_ident = const.tile([P, P], F32)
         nc.vector.tensor_scalar(out=half_ident[:], in0=ident[:], scalar1=0.5, scalar2=None, op0=ALU.mult)
         g2 = const.tile([P, 1], F32)
@@ -78,17 +85,19 @@ def tile_rbf_svm_kernel(tc, X, SV, DC, IC, gamma, out):
         nc.vector.tensor_copy(out=ic_f[:], in_=ic_bf[:])
 
         x2col = keep.tile([P, NB], F32)
-        hx2 = keep.tile([P, NB], F32)
-        sv2col = keep.tile([P, M_ROWS // P], F32)
-        hsv2b = keep.tile([P, M_ROWS], F32)
-        acc = keep.tile([P, NB * n_groups], F32)
+        hx2b = keep.tile([P, N_ROWS], F32)
+        sv2col = keep.tile([P, N_SVT], F32)
+        hsv2col = keep.tile([P, N_SVT], F32)
+        dccol = keep.tile([P, N_SVT], F32)
 
         xq = keep.tile([P, N_ROWS], U32, align_bytes=64)
         xs = keep.tile([P, N_ROWS], U8, align_bytes=64)
         svq = keep.tile([P, M_ROWS], U32, align_bytes=64)
         svs = keep.tile([P, M_ROWS], U8, align_bytes=64)
 
-        def transpose_group(src_f32, n_tiles, grouped_f32, on_vector):
+        red = ps_r.tile([P, N_SVT * NB], F32)
+
+        def transpose_group(src_f32, n_tiles, grouped_f32):
             for pair in range(n_tiles // 2):
                 xt = ps_t.tile([P, 4, P], F32, name="xt")
                 for jj in range(2):
@@ -98,85 +107,92 @@ def tile_rbf_svm_kernel(tc, X, SV, DC, IC, gamma, out):
                 dst = grouped_f32[:, pair * 512:(pair + 1) * 512].rearrange(
                     "p (j r u) -> p j r u", j=2, u=2)
                 src = xt[:].rearrange("p (j u) r -> p j r u", j=2)
-                if on_vector:
-                    nc.vector.tensor_copy(out=dst, in_=src)
-                else:
-                    nc.scalar.copy(out=dst, in_=src)
+                nc.vector.tensor_copy(out=dst, in_=src)
 
         def square_sum(src, col):
             junk = junkp.tile([P, D], BF16, name="junk")
             nc.scalar.activation(out=junk[:], in_=src, func=ACT.Square, accum_out=col)
 
-        gx = keep.tile([P, N_ROWS * 4], BF16, align_bytes=64)
-        transpose_group(x_nat[:].bitcast(F32), NB, gx[:].bitcast(F32), True)
-        nc.vector.quantize_mx(out=xq[:].bitcast(FP8X4), scales=xs[:], in_=gx[:])
-
-        def prep_x_norm(j):
+        for j in range(NB):
             square_sum(x_nat[:, j * D:(j + 1) * D], x2col[:, j:j + 1])
-            nc.vector.tensor_scalar(out=hx2[:, j:j + 1], in0=x2col[:, j:j + 1], scalar1=0.5,
-                                    scalar2=None, op0=ALU.mult)
+        gx = keep.tile([P, N_ROWS * 4], BF16, align_bytes=64)
+        transpose_group(x_nat[:].bitcast(F32), NB, gx[:].bitcast(F32))
+        nc.vector.quantize_mx(out=xq[:].bitcast(FP8X4), scales=xs[:], in_=gx[:])
+        for h in range(N_ROWS // HALF):
+            bc = ps_t.tile([P, HALF], F32, name="xt")
+            for jj in range(HALF // P):
+                j = h * (HALF // P) + jj
+                nc.tensor.matmul(out=bc[:, jj * P:(jj + 1) * P],
+                                 lhsT=x2col[:, j:j + 1].to_broadcast([P, P]),
+                                 rhs=half_ident[:], start=True, stop=True)
+            nc.vector.tensor_copy(out=hx2b[:, h * HALF:(h + 1) * HALF], in_=bc[:])
 
-        def prep_sv(mb, on_vector):
+        dct = ps_t.tile([P, P], BF16, name="xt")
+        nc.tensor.transpose(dct[:], dc_rows[:], ident_bf[:])
+        nc.vector.tensor_copy(out=dccol[:], in_=dct[:, 0:N_SVT])
+
+        def prep_sv(mb):
             t = sv_nat[mb]
             cols = slice(mb * MB_COLS, (mb + 1) * MB_COLS)
+            c0 = mb * TILES_PER_MB
             for j in range(TILES_PER_MB):
-                c = mb * TILES_PER_MB + j
-                square_sum(t[:, j * D:(j + 1) * D], sv2col[:, c:c + 1])
+                square_sum(t[:, j * D:(j + 1) * D], sv2col[:, c0 + j:c0 + j + 1])
+            nc.vector.tensor_scalar(out=hsv2col[:, c0:c0 + TILES_PER_MB], in0=sv2col[:, c0:c0 + TILES_PER_MB],
+                                    scalar1=0.5, scalar2=None, op0=ALU.mult)
             grouped = stage.tile([P, MB_COLS * 4], BF16, align_bytes=64, name="grouped")
-            transpose_group(t[:].bitcast(F32), TILES_PER_MB, grouped[:].bitcast(F32), on_vector)
+            transpose_group(t[:].bitcast(F32), TILES_PER_MB, grouped[:].bitcast(F32))
             nc.vector.quantize_mx(out=svq[:, cols].bitcast(FP8X4), scales=svs[:, cols], in_=grouped[:])
-            bc = ps_b.tile([P, MB_COLS], F32, name="bc")
-            for j in range(TILES_PER_MB):
-                c = mb * TILES_PER_MB + j
-                nc.tensor.matmul(out=bc[:, j * P:(j + 1) * P],
-                                 lhsT=sv2col[:, c:c + 1].to_broadcast([P, P]),
-                                 rhs=half_ident[:], start=True, stop=True)
-            nc.scalar.copy(out=hsv2b[:, cols], in_=bc[:])
-            if mb + 2 < N_MB:
-                load_sv(mb + 2)
+            if mb + 3 < N_MB:
+                load_sv(mb + 3)
 
-        def main_step(g, nb):
-            mbs = GROUPS[g]
-            width = len(mbs) * MB_COLS
-            w = work.tile([P, 4 * MB_COLS], F32, name="w")
-            for i, mb in enumerate(mbs):
-                cols = slice(mb * MB_COLS, (mb + 1) * MB_COLS)
-                ps = ps_mm.tile([P, MB_COLS], F32, name="ps")
-                nc.tensor.matmul_mx(
-                    out=ps[:],
-                    lhsT=xq[:, nb * P:(nb + 1) * P].bitcast(FP8X4),
-                    lhsT_scale=xs[:, nb * P:(nb + 1) * P],
-                    rhs=svq[:, cols].bitcast(FP8X4),
-                    rhs_scale=svs[:, cols],
-                    start=True, stop=True,
-                )
-                nc.vector.scalar_tensor_tensor(
-                    out=w[:, i * MB_COLS:(i + 1) * MB_COLS], in0=ps[:], scalar=hx2[:, nb:nb + 1],
-                    in1=hsv2b[:, cols], op0=ALU.subtract, op1=ALU.subtract)
-            nc.scalar.activation(out=w[:, :width], in_=w[:, :width], func=ACT.Exp, scale=g2[:, 0:1])
-            c0 = mbs[0] * MB_COLS
-            k = nb * n_groups + g
-            nc.vector.scalar_tensor_tensor(
-                out=w[:, :width], in0=w[:, :width], scalar=1.0, in1=dcb[:, c0:c0 + width],
-                op0=ALU.min, op1=ALU.mult, accum_out=acc[:, k:k + 1])
+        w_tiles = {}
 
-        prep_x_norm(0)
-        prep_sv(0, True)
-        for j in range(1, NB):
-            prep_x_norm(j)
+        def front(i):
+            w = work.tile([P, SVT_PER_W * N_ROWS], F32, name="w")
+            w_tiles[i] = w
+            for s in range(SVT_PER_W):
+                t = i * SVT_PER_W + s
+                for h in range(N_ROWS // HALF):
+                    ps = ps_mm.tile([P, HALF], F32, name="ps")
+                    nc.tensor.matmul_mx(
+                        out=ps[:],
+                        lhsT=svq[:, t * P:(t + 1) * P].bitcast(FP8X4),
+                        lhsT_scale=svs[:, t * P:(t + 1) * P],
+                        rhs=xq[:, h * HALF:(h + 1) * HALF].bitcast(FP8X4),
+                        rhs_scale=xs[:, h * HALF:(h + 1) * HALF],
+                        start=True, stop=True,
+                    )
+                    o = s * N_ROWS + h * HALF
+                    nc.vector.scalar_tensor_tensor(
+                        out=w[:, o:o + HALF], in0=ps[:], scalar=hsv2col[:, t:t + 1],
+                        in1=hx2b[:, h * HALF:(h + 1) * HALF], op0=ALU.subtract, op1=ALU.subtract)
+            nc.gpsimd.tensor_scalar(out=w[:], in0=w[:], scalar1=0.0, scalar2=-3.0e38,
+                                    op0=ALU.min, op1=ALU.max)
+            nc.scalar.activation(out=w[:], in_=w[:], func=ACT.Exp, scale=g2[:, 0:1])
 
-        for g in range(n_groups):
-            nxt = GROUPS[g + 1] if g + 1 < n_groups else []
-            when = {}
-            for i, mb in enumerate(nxt):
-                when[(i * NB) // len(nxt)] = when.get((i * NB) // len(nxt), []) + [mb]
-            for nb in range(NB):
-                for mb in when.get(nb, []):
-                    prep_sv(mb, False)
-                main_step(g, nb)
+        def back(i):
+            w = w_tiles[i]
+            for s in range(SVT_PER_W):
+                t = i * SVT_PER_W + s
+                for j in range(NB):
+                    o = s * N_ROWS + j * P
+                    k = t * NB + j
+                    nc.tensor.matmul(out=red[:, k:k + 1], lhsT=w[:, o:o + P], rhs=dccol[:, t:t + 1],
+                                     start=True, stop=True)
+
+        prep_sv(0)
+        prep_sv(1)
+        w_per_mb = TILES_PER_MB // SVT_PER_W
+        for i in range(N_W + LAG):
+            if i < N_W:
+                if i % w_per_mb == 0 and i // w_per_mb + 2 < N_MB:
+                    prep_sv(i // w_per_mb + 2)
+                front(i)
+            if i >= LAG:
+                back(i - LAG)
 
         res = const.tile([P, NB], F32)
-        nc.vector.tensor_reduce(out=res[:], in_=acc[:].rearrange("p (j g) -> p j g", g=n_groups),
+        nc.vector.tensor_reduce(out=res[:], in_=red[:].rearrange("p (t j) -> p j t", j=NB),
                                 axis=AX.X, op=ALU.add)
         res2 = const.tile([P, NB], F32)
         nc.vector.tensor_scalar(out=res2[:], in0=res[:], scalar1=ic_f[:, 0:1], scalar2=None, op0=ALU.add)

@@ -25,7 +25,7 @@ TILES_PER_MB = MB_COLS // P
 N_SVT = M_ROWS // P
 SVT_PER_W = 2
 N_W = N_SVT // SVT_PER_W
-LAG = 2
+LAG = 3
 
 FLOPS = 2 * N_ROWS * M_ROWS * D
 
@@ -97,7 +97,7 @@ def tile_rbf_svm_kernel(tc, X, SV, DC, IC, gamma, out):
 
         red = ps_r.tile([P, N_SVT * NB], F32)
 
-        def transpose_group(src_f32, n_tiles, grouped_f32):
+        def transpose_group(src_f32, n_tiles, grouped_f32, on_vector):
             for pair in range(n_tiles // 2):
                 xt = ps_t.tile([P, 4, P], F32, name="xt")
                 for jj in range(2):
@@ -107,23 +107,32 @@ def tile_rbf_svm_kernel(tc, X, SV, DC, IC, gamma, out):
                 dst = grouped_f32[:, pair * 512:(pair + 1) * 512].rearrange(
                     "p (j r u) -> p j r u", j=2, u=2)
                 src = xt[:].rearrange("p (j u) r -> p j r u", j=2)
-                nc.vector.tensor_copy(out=dst, in_=src)
+                if on_vector[pair]:
+                    nc.vector.tensor_copy(out=dst, in_=src)
+                else:
+                    nc.scalar.copy(out=dst, in_=src)
 
         def square_sum(src, col):
             junk = junkp.tile([P, D], BF16, name="junk")
             nc.scalar.activation(out=junk[:], in_=src, func=ACT.Square, accum_out=col)
 
-        for j in range(NB):
+        for j in range(NB // 2):
             square_sum(x_nat[:, j * D:(j + 1) * D], x2col[:, j:j + 1])
         gx = keep.tile([P, N_ROWS * 4], BF16, align_bytes=64)
-        transpose_group(x_nat[:].bitcast(F32), NB, gx[:].bitcast(F32))
+        transpose_group(x_nat[:].bitcast(F32), NB, gx[:].bitcast(F32), [True] * (NB // 2))
         nc.vector.quantize_mx(out=xq[:].bitcast(FP8X4), scales=xs[:], in_=gx[:])
+        x2col_v = keep.tile([P, NB], F32)
+        for j in range(NB // 2, NB):
+            junk = junkp.tile([P, D], F32, name="junk_v")
+            nc.vector.scalar_tensor_tensor(
+                out=junk[:], in0=x_nat[:, j * D:(j + 1) * D], scalar=1.0, in1=x_nat[:, j * D:(j + 1) * D],
+                op0=ALU.mult, op1=ALU.mult, accum_out=x2col_v[:, j:j + 1])
         for h in range(N_ROWS // HALF):
             bc = ps_t.tile([P, HALF], F32, name="xt")
             for jj in range(HALF // P):
                 j = h * (HALF // P) + jj
                 nc.tensor.matmul(out=bc[:, jj * P:(jj + 1) * P],
-                                 lhsT=x2col[:, j:j + 1].to_broadcast([P, P]),
+                                 lhsT=(x2col if h == 0 else x2col_v)[:, j:j + 1].to_broadcast([P, P]),
                                  rhs=half_ident[:], start=True, stop=True)
             nc.vector.tensor_copy(out=hx2b[:, h * HALF:(h + 1) * HALF], in_=bc[:])
 
@@ -140,7 +149,8 @@ def tile_rbf_svm_kernel(tc, X, SV, DC, IC, gamma, out):
             nc.vector.tensor_scalar(out=hsv2col[:, c0:c0 + TILES_PER_MB], in0=sv2col[:, c0:c0 + TILES_PER_MB],
                                     scalar1=0.5, scalar2=None, op0=ALU.mult)
             grouped = stage.tile([P, MB_COLS * 4], BF16, align_bytes=64, name="grouped")
-            transpose_group(t[:].bitcast(F32), TILES_PER_MB, grouped[:].bitcast(F32))
+            transpose_group(t[:].bitcast(F32), TILES_PER_MB, grouped[:].bitcast(F32),
+                            [mb < 1 or mb % 2 == 1, mb < 1])
             nc.vector.quantize_mx(out=svq[:, cols].bitcast(FP8X4), scales=svs[:, cols], in_=grouped[:])
             if mb + 3 < N_MB:
                 load_sv(mb + 3)
@@ -166,8 +176,7 @@ def tile_rbf_svm_kernel(tc, X, SV, DC, IC, gamma, out):
                     nc.vector.scalar_tensor_tensor(
                         out=w[:, o:o + HALF], in0=ps[:], scalar=hsv2col[:, t:t + 1],
                         in1=hx2b[:, h * HALF:(h + 1) * HALF], op0=ALU.subtract, op1=ALU.subtract)
-            nc.gpsimd.tensor_scalar(out=w[:], in0=w[:], scalar1=0.0, scalar2=-3.0e38,
-                                    op0=ALU.min, op1=ALU.max)
+            nc.vector.tensor_scalar(out=w[:], in0=w[:], scalar1=0.0, scalar2=None, op0=ALU.min)
             nc.scalar.activation(out=w[:], in_=w[:], func=ACT.Exp, scale=g2[:, 0:1])
 
         def back(i):

@@ -18,20 +18,17 @@ M_ROWS = 8192
 D = 512
 WORDS = D // 2
 NB = N_ROWS // P
-HALF = 512
 MB_COLS = 512
 N_MB = M_ROWS // MB_COLS
 TILES_PER_MB = MB_COLS // P
-N_SVT = M_ROWS // P
-SVT_PER_W = 2
-N_W = N_SVT // SVT_PER_W
-LAG = 3
+GROUPS = [[0], [1], [2, 3], [4, 5, 6, 7], [8, 9, 10, 11], [12, 13, 14, 15]]
 
 FLOPS = 2 * N_ROWS * M_ROWS * D
 
 
 def tile_rbf_svm_kernel(tc, X, SV, DC, IC, gamma, out):
     nc = tc.nc
+    n_groups = len(GROUPS)
     with ExitStack() as ctx:
         const = ctx.enter_context(tc.tile_pool(name="const", bufs=1))
         keep = ctx.enter_context(tc.tile_pool(name="keep", bufs=1))
@@ -40,8 +37,8 @@ def tile_rbf_svm_kernel(tc, X, SV, DC, IC, gamma, out):
         work = ctx.enter_context(tc.tile_pool(name="work", bufs=6))
         junkp = ctx.enter_context(tc.tile_pool(name="junkp", bufs=2))
         ps_mm = ctx.enter_context(tc.psum_pool(name="ps_mm", bufs=4))
-        ps_t = ctx.enter_context(tc.psum_pool(name="ps_t", bufs=3))
-        ps_r = ctx.enter_context(tc.psum_pool(name="ps_r", bufs=1))
+        ps_t = ctx.enter_context(tc.psum_pool(name="ps_t", bufs=2))
+        ps_b = ctx.enter_context(tc.psum_pool(name="ps_b", bufs=2))
 
         x_nat = keep.tile([P, NB * D], BF16)
         nc.sync.dma_start(
@@ -52,9 +49,6 @@ def tile_rbf_svm_kernel(tc, X, SV, DC, IC, gamma, out):
         nc.scalar.dma_start(out=g_bf[:], in_=gamma.partition_broadcast(P))
         ic_bf = const.tile([P, 1], BF16)
         nc.scalar.dma_start(out=ic_bf[:], in_=IC.partition_broadcast(P))
-        dc_rows = const.tile([P, P], BF16)
-        nc.vector.memset(dc_rows[:], 0.0)
-        nc.scalar.dma_start(out=dc_rows[0:N_SVT, :], in_=DC.rearrange("o (t p) -> (o t) p", p=P))
 
         sv_nat = {}
 
@@ -68,15 +62,14 @@ def tile_rbf_svm_kernel(tc, X, SV, DC, IC, gamma, out):
 
         load_sv(0)
         load_sv(1)
-        load_sv(2)
+        dcb = keep.tile([P, M_ROWS], BF16)
+        nc.scalar.dma_start(out=dcb[:], in_=DC.rearrange("o m -> (o m)").partition_broadcast(P))
 
         warm = const.tile([P, 1], F32)
         nc.vector.memset(warm[:], 0.0)
         nc.scalar.activation(out=warm[:], in_=warm[:], func=ACT.Exp)
         ident = const.tile([P, P], F32)
         make_identity(nc, ident[:])
-        ident_bf = const.tile([P, P], BF16)
-        nc.vector.tensor_copy(out=ident_bf[:], in_=ident[:])
         half_ident = const.tile([P, P], F32)
         nc.vector.tensor_scalar(out=half_ident[:], in0=ident[:], scalar1=0.5, scalar2=None, op0=ALU.mult)
         g2 = const.tile([P, 1], F32)
@@ -85,17 +78,15 @@ def tile_rbf_svm_kernel(tc, X, SV, DC, IC, gamma, out):
         nc.vector.tensor_copy(out=ic_f[:], in_=ic_bf[:])
 
         x2col = keep.tile([P, NB], F32)
-        hx2b = keep.tile([P, N_ROWS], F32)
-        sv2col = keep.tile([P, N_SVT], F32)
-        hsv2col = keep.tile([P, N_SVT], F32)
-        dccol = keep.tile([P, N_SVT], F32)
+        hx2 = keep.tile([P, NB], F32)
+        sv2col = keep.tile([P, M_ROWS // P], F32)
+        hsv2b = keep.tile([P, M_ROWS], F32)
+        acc = keep.tile([P, NB * n_groups], F32)
 
         xq = keep.tile([P, N_ROWS], U32, align_bytes=64)
         xs = keep.tile([P, N_ROWS], U8, align_bytes=64)
         svq = keep.tile([P, M_ROWS], U32, align_bytes=64)
         svs = keep.tile([P, M_ROWS], U8, align_bytes=64)
-
-        red = ps_r.tile([P, N_SVT * NB], F32)
 
         def transpose_group(src_f32, n_tiles, grouped_f32, on_vector):
             for pair in range(n_tiles // 2):
@@ -107,7 +98,7 @@ def tile_rbf_svm_kernel(tc, X, SV, DC, IC, gamma, out):
                 dst = grouped_f32[:, pair * 512:(pair + 1) * 512].rearrange(
                     "p (j r u) -> p j r u", j=2, u=2)
                 src = xt[:].rearrange("p (j u) r -> p j r u", j=2)
-                if on_vector[pair]:
+                if on_vector:
                     nc.vector.tensor_copy(out=dst, in_=src)
                 else:
                     nc.scalar.copy(out=dst, in_=src)
@@ -116,92 +107,78 @@ def tile_rbf_svm_kernel(tc, X, SV, DC, IC, gamma, out):
             junk = junkp.tile([P, D], BF16, name="junk")
             nc.scalar.activation(out=junk[:], in_=src, func=ACT.Square, accum_out=col)
 
-        for j in range(NB // 2):
-            square_sum(x_nat[:, j * D:(j + 1) * D], x2col[:, j:j + 1])
         gx = keep.tile([P, N_ROWS * 4], BF16, align_bytes=64)
-        transpose_group(x_nat[:].bitcast(F32), NB, gx[:].bitcast(F32), [True] * (NB // 2))
+        transpose_group(x_nat[:].bitcast(F32), NB, gx[:].bitcast(F32), True)
         nc.vector.quantize_mx(out=xq[:].bitcast(FP8X4), scales=xs[:], in_=gx[:])
-        x2col_v = keep.tile([P, NB], F32)
-        for j in range(NB // 2, NB):
-            junk = junkp.tile([P, D], F32, name="junk_v")
-            nc.vector.scalar_tensor_tensor(
-                out=junk[:], in0=x_nat[:, j * D:(j + 1) * D], scalar=1.0, in1=x_nat[:, j * D:(j + 1) * D],
-                op0=ALU.mult, op1=ALU.mult, accum_out=x2col_v[:, j:j + 1])
-        for h in range(N_ROWS // HALF):
-            bc = ps_t.tile([P, HALF], F32, name="xt")
-            for jj in range(HALF // P):
-                j = h * (HALF // P) + jj
-                nc.tensor.matmul(out=bc[:, jj * P:(jj + 1) * P],
-                                 lhsT=(x2col if h == 0 else x2col_v)[:, j:j + 1].to_broadcast([P, P]),
-                                 rhs=half_ident[:], start=True, stop=True)
-            nc.vector.tensor_copy(out=hx2b[:, h * HALF:(h + 1) * HALF], in_=bc[:])
 
-        dct = ps_t.tile([P, P], BF16, name="xt")
-        nc.tensor.transpose(dct[:], dc_rows[:], ident_bf[:])
-        nc.vector.tensor_copy(out=dccol[:], in_=dct[:, 0:N_SVT])
+        def prep_x_norm(j):
+            square_sum(x_nat[:, j * D:(j + 1) * D], x2col[:, j:j + 1])
+            nc.vector.tensor_scalar(out=hx2[:, j:j + 1], in0=x2col[:, j:j + 1], scalar1=0.5,
+                                    scalar2=None, op0=ALU.mult)
 
-        def prep_sv(mb):
+        def prep_sv(mb, on_vector):
             t = sv_nat[mb]
             cols = slice(mb * MB_COLS, (mb + 1) * MB_COLS)
-            c0 = mb * TILES_PER_MB
             for j in range(TILES_PER_MB):
-                square_sum(t[:, j * D:(j + 1) * D], sv2col[:, c0 + j:c0 + j + 1])
-            nc.vector.tensor_scalar(out=hsv2col[:, c0:c0 + TILES_PER_MB], in0=sv2col[:, c0:c0 + TILES_PER_MB],
-                                    scalar1=0.5, scalar2=None, op0=ALU.mult)
+                c = mb * TILES_PER_MB + j
+                square_sum(t[:, j * D:(j + 1) * D], sv2col[:, c:c + 1])
             grouped = stage.tile([P, MB_COLS * 4], BF16, align_bytes=64, name="grouped")
-            transpose_group(t[:].bitcast(F32), TILES_PER_MB, grouped[:].bitcast(F32),
-                            [mb < 1 or mb % 2 == 1, mb < 1])
+            transpose_group(t[:].bitcast(F32), TILES_PER_MB, grouped[:].bitcast(F32), on_vector)
             nc.vector.quantize_mx(out=svq[:, cols].bitcast(FP8X4), scales=svs[:, cols], in_=grouped[:])
-            if mb + 3 < N_MB:
-                load_sv(mb + 3)
+            bc = ps_b.tile([P, MB_COLS], F32, name="bc")
+            for j in range(TILES_PER_MB):
+                c = mb * TILES_PER_MB + j
+                nc.tensor.matmul(out=bc[:, j * P:(j + 1) * P],
+                                 lhsT=sv2col[:, c:c + 1].to_broadcast([P, P]),
+                                 rhs=half_ident[:], start=True, stop=True)
+            nc.scalar.copy(out=hsv2b[:, cols], in_=bc[:])
+            if mb + 2 < N_MB:
+                load_sv(mb + 2)
 
-        w_tiles = {}
+        def main_step(g, nb):
+            mbs = GROUPS[g]
+            width = len(mbs) * MB_COLS
+            w = work.tile([P, 4 * MB_COLS], F32, name="w")
+            for i, mb in enumerate(mbs):
+                cols = slice(mb * MB_COLS, (mb + 1) * MB_COLS)
+                ps = ps_mm.tile([P, MB_COLS], F32, name="ps")
+                nc.tensor.matmul_mx(
+                    out=ps[:],
+                    lhsT=xq[:, nb * P:(nb + 1) * P].bitcast(FP8X4),
+                    lhsT_scale=xs[:, nb * P:(nb + 1) * P],
+                    rhs=svq[:, cols].bitcast(FP8X4),
+                    rhs_scale=svs[:, cols],
+                    start=True, stop=True,
+                )
+                nc.vector.scalar_tensor_tensor(
+                    out=w[:, i * MB_COLS:(i + 1) * MB_COLS], in0=ps[:], scalar=hx2[:, nb:nb + 1],
+                    in1=hsv2b[:, cols], op0=ALU.subtract, op1=ALU.subtract)
+            nc.gpsimd.tensor_scalar(out=w[:, :width], in0=w[:, :width], scalar1=0.0, scalar2=-3.0e38,
+                                    op0=ALU.min, op1=ALU.max)
+            nc.scalar.activation(out=w[:, :width], in_=w[:, :width], func=ACT.Exp, scale=g2[:, 0:1])
+            c0 = mbs[0] * MB_COLS
+            k = nb * n_groups + g
+            nc.vector.scalar_tensor_tensor(
+                out=w[:, :width], in0=w[:, :width], scalar=1.0, in1=dcb[:, c0:c0 + width],
+                op0=ALU.mult, op1=ALU.mult, accum_out=acc[:, k:k + 1])
 
-        def front(i):
-            w = work.tile([P, SVT_PER_W * N_ROWS], F32, name="w")
-            w_tiles[i] = w
-            for s in range(SVT_PER_W):
-                t = i * SVT_PER_W + s
-                for h in range(N_ROWS // HALF):
-                    ps = ps_mm.tile([P, HALF], F32, name="ps")
-                    nc.tensor.matmul_mx(
-                        out=ps[:],
-                        lhsT=svq[:, t * P:(t + 1) * P].bitcast(FP8X4),
-                        lhsT_scale=svs[:, t * P:(t + 1) * P],
-                        rhs=xq[:, h * HALF:(h + 1) * HALF].bitcast(FP8X4),
-                        rhs_scale=xs[:, h * HALF:(h + 1) * HALF],
-                        start=True, stop=True,
-                    )
-                    o = s * N_ROWS + h * HALF
-                    nc.vector.scalar_tensor_tensor(
-                        out=w[:, o:o + HALF], in0=ps[:], scalar=hsv2col[:, t:t + 1],
-                        in1=hx2b[:, h * HALF:(h + 1) * HALF], op0=ALU.subtract, op1=ALU.subtract)
-            nc.vector.tensor_scalar(out=w[:], in0=w[:], scalar1=0.0, scalar2=None, op0=ALU.min)
-            nc.scalar.activation(out=w[:], in_=w[:], func=ACT.Exp, scale=g2[:, 0:1])
+        prep_x_norm(0)
+        prep_sv(0, True)
+        for j in range(1, NB):
+            prep_x_norm(j)
 
-        def back(i):
-            w = w_tiles[i]
-            for s in range(SVT_PER_W):
-                t = i * SVT_PER_W + s
-                for j in range(NB):
-                    o = s * N_ROWS + j * P
-                    k = t * NB + j
-                    nc.tensor.matmul(out=red[:, k:k + 1], lhsT=w[:, o:o + P], rhs=dccol[:, t:t + 1],
-                                     start=True, stop=True)
-
-        prep_sv(0)
-        prep_sv(1)
-        w_per_mb = TILES_PER_MB // SVT_PER_W
-        for i in range(N_W + LAG):
-            if i < N_W:
-                if i % w_per_mb == 0 and i // w_per_mb + 2 < N_MB:
-                    prep_sv(i // w_per_mb + 2)
-                front(i)
-            if i >= LAG:
-                back(i - LAG)
+        for g in range(n_groups):
+            nxt = GROUPS[g + 1] if g + 1 < n_groups else []
+            when = {}
+            for i, mb in enumerate(nxt):
+                when[(i * NB) // len(nxt)] = when.get((i * NB) // len(nxt), []) + [mb]
+            for nb in range(NB):
+                for mb in when.get(nb, []):
+                    prep_sv(mb, False)
+                main_step(g, nb)
 
         res = const.tile([P, NB], F32)
-        nc.vector.tensor_reduce(out=res[:], in_=red[:].rearrange("p (t j) -> p j t", j=NB),
+        nc.vector.tensor_reduce(out=res[:], in_=acc[:].rearrange("p (j g) -> p j g", g=n_groups),
                                 axis=AX.X, op=ALU.add)
         res2 = const.tile([P, NB], F32)
         nc.vector.tensor_scalar(out=res2[:], in0=res[:], scalar1=ic_f[:, 0:1], scalar2=None, op0=ALU.add)

@@ -18,17 +18,20 @@ M_ROWS = 8192
 D = 512
 WORDS = D // 2
 NB = N_ROWS // P
+HALF = 512
 MB_COLS = 512
 N_MB = M_ROWS // MB_COLS
 TILES_PER_MB = MB_COLS // P
-GROUPS = [[0], [1], [2, 3], [4, 5, 6, 7], [8, 9, 10, 11], [12, 13, 14, 15]]
+N_SVT = M_ROWS // P
+SVT_PER_W = 2
+N_W = N_SVT // SVT_PER_W
+LAG = 2
 
 FLOPS = 2 * N_ROWS * M_ROWS * D
 
 
 def tile_rbf_svm_kernel(tc, X, SV, DC, IC, gamma, out):
     nc = tc.nc
-    n_groups = len(GROUPS)
     with ExitStack() as ctx:
         const = ctx.enter_context(tc.tile_pool(name="const", bufs=1))
         keep = ctx.enter_context(tc.tile_pool(name="keep", bufs=1))
@@ -38,7 +41,7 @@ def tile_rbf_svm_kernel(tc, X, SV, DC, IC, gamma, out):
         junkp = ctx.enter_context(tc.tile_pool(name="junkp", bufs=2))
         ps_mm = ctx.enter_context(tc.psum_pool(name="ps_mm", bufs=4))
         ps_t = ctx.enter_context(tc.psum_pool(name="ps_t", bufs=2))
-        ps_b = ctx.enter_context(tc.psum_pool(name="ps_b", bufs=2))
+        ps_r = ctx.enter_context(tc.psum_pool(name="ps_r", bufs=1))
 
         x_nat = keep.tile([P, NB * D], BF16)
         nc.sync.dma_start(
@@ -49,6 +52,9 @@ def tile_rbf_svm_kernel(tc, X, SV, DC, IC, gamma, out):
         nc.scalar.dma_start(out=g_bf[:], in_=gamma.partition_broadcast(P))
         ic_bf = const.tile([P, 1], BF16)
         nc.scalar.dma_start(out=ic_bf[:], in_=IC.partition_broadcast(P))
+        dc_rows = const.tile([P, P], BF16)
+        nc.vector.memset(dc_rows[:], 0.0)
+        nc.scalar.dma_start(out=dc_rows[0:N_SVT, :], in_=DC.rearrange("o (t p) -> (o t) p", p=P))
 
         sv_nat = {}
 
@@ -62,14 +68,15 @@ def tile_rbf_svm_kernel(tc, X, SV, DC, IC, gamma, out):
 
         load_sv(0)
         load_sv(1)
-        dcb = keep.tile([P, M_ROWS], BF16)
-        nc.scalar.dma_start(out=dcb[:], in_=DC.rearrange("o m -> (o m)").partition_broadcast(P))
+        load_sv(2)
 
         warm = const.tile([P, 1], F32)
         nc.vector.memset(warm[:], 0.0)
         nc.scalar.activation(out=warm[:], in_=warm[:], func=ACT.Exp)
         ident = const.tile([P, P], F32)
         make_identity(nc, ident[:])
+        ident_bf = const.tile([P, P], BF16)
+        nc.vector.tensor_copy(out=ident_bf[:], in_=ident[:])
         half_ident = const.tile([P, P], F32)
         nc.vector.tensor_scalar(out=half_ident[:], in0=ident[:], scalar1=0.5, scalar2=None, op0=ALU.mult)
         g2 = const.tile([P, 1], F32)
@@ -78,15 +85,17 @@ def tile_rbf_svm_kernel(tc, X, SV, DC, IC, gamma, out):
         nc.vector.tensor_copy(out=ic_f[:], in_=ic_bf[:])
 
         x2col = keep.tile([P, NB], F32)
-        hx2 = keep.tile([P, NB], F32)
-        sv2col = keep.tile([P, M_ROWS // P], F32)
-        hsv2b = keep.tile([P, M_ROWS], F32)
-        acc = keep.tile([P, NB * n_groups], F32)
+        hx2b = keep.tile([P, N_ROWS], F32)
+        sv2col = keep.tile([P, N_SVT], F32)
+        hsv2col = keep.tile([P, N_SVT], F32)
+        dccol = keep.tile([P, N_SVT], F32)
 
         xq = keep.tile([P, N_ROWS], U32, align_bytes=64)
         xs = keep.tile([P, N_ROWS], U8, align_bytes=64)
         svq = keep.tile([P, M_ROWS], U32, align_bytes=64)
         svs = keep.tile([P, M_ROWS], U8, align_bytes=64)
+
+        acc = [ps_r.tile([P, HALF // P, P], F32, name="acc%d" % h) for h in range(N_ROWS // HALF)]
 
         def transpose_group(src_f32, n_tiles, grouped_f32, on_vector):
             for pair in range(n_tiles // 2):
@@ -98,7 +107,7 @@ def tile_rbf_svm_kernel(tc, X, SV, DC, IC, gamma, out):
                 dst = grouped_f32[:, pair * 512:(pair + 1) * 512].rearrange(
                     "p (j r u) -> p j r u", j=2, u=2)
                 src = xt[:].rearrange("p (j u) r -> p j r u", j=2)
-                if on_vector:
+                if on_vector[pair]:
                     nc.vector.tensor_copy(out=dst, in_=src)
                 else:
                     nc.scalar.copy(out=dst, in_=src)
@@ -107,79 +116,105 @@ def tile_rbf_svm_kernel(tc, X, SV, DC, IC, gamma, out):
             junk = junkp.tile([P, D], BF16, name="junk")
             nc.scalar.activation(out=junk[:], in_=src, func=ACT.Square, accum_out=col)
 
-        gx = keep.tile([P, N_ROWS * 4], BF16, align_bytes=64)
-        transpose_group(x_nat[:].bitcast(F32), NB, gx[:].bitcast(F32), True)
-        nc.vector.quantize_mx(out=xq[:].bitcast(FP8X4), scales=xs[:], in_=gx[:])
-
-        def prep_x_norm(j):
+        for j in range(NB // 2):
             square_sum(x_nat[:, j * D:(j + 1) * D], x2col[:, j:j + 1])
-            nc.vector.tensor_scalar(out=hx2[:, j:j + 1], in0=x2col[:, j:j + 1], scalar1=0.5,
-                                    scalar2=None, op0=ALU.mult)
+        gx = keep.tile([P, N_ROWS * 4], BF16, align_bytes=64)
+        transpose_group(x_nat[:].bitcast(F32), NB, gx[:].bitcast(F32), [True] * (NB // 2))
+        nc.vector.quantize_mx(out=xq[:].bitcast(FP8X4), scales=xs[:], in_=gx[:])
+        x2col_v = keep.tile([P, NB], F32)
+        for j in range(NB // 2, NB):
+            junk = junkp.tile([P, D], F32, name="junk_v")
+            nc.vector.scalar_tensor_tensor(
+                out=junk[:], in0=x_nat[:, j * D:(j + 1) * D], scalar=1.0, in1=x_nat[:, j * D:(j + 1) * D],
+                op0=ALU.mult, op1=ALU.mult, accum_out=x2col_v[:, j:j + 1])
+        for h in range(N_ROWS // HALF):
+            bc = ps_t.tile([P, HALF], F32, name="xt")
+            for jj in range(HALF // P):
+                j = h * (HALF // P) + jj
+                nc.tensor.matmul(out=bc[:, jj * P:(jj + 1) * P],
+                                 lhsT=(x2col if h == 0 else x2col_v)[:, j:j + 1].to_broadcast([P, P]),
+                                 rhs=half_ident[:], start=True, stop=True)
+            nc.vector.tensor_copy(out=hx2b[:, h * HALF:(h + 1) * HALF], in_=bc[:])
 
-        def prep_sv(mb, on_vector):
+        dct = ps_t.tile([P, P], BF16, name="xt")
+        nc.tensor.transpose(dct[:], dc_rows[:], ident_bf[:])
+        nc.vector.tensor_copy(out=dccol[:], in_=dct[:, 0:N_SVT])
+
+        def prep_sv(mb):
             t = sv_nat[mb]
             cols = slice(mb * MB_COLS, (mb + 1) * MB_COLS)
+            c0 = mb * TILES_PER_MB
             for j in range(TILES_PER_MB):
-                c = mb * TILES_PER_MB + j
-                square_sum(t[:, j * D:(j + 1) * D], sv2col[:, c:c + 1])
+                square_sum(t[:, j * D:(j + 1) * D], sv2col[:, c0 + j:c0 + j + 1])
+            nc.vector.tensor_scalar(out=hsv2col[:, c0:c0 + TILES_PER_MB], in0=sv2col[:, c0:c0 + TILES_PER_MB],
+                                    scalar1=0.5, scalar2=None, op0=ALU.mult)
             grouped = stage.tile([P, MB_COLS * 4], BF16, align_bytes=64, name="grouped")
-            transpose_group(t[:].bitcast(F32), TILES_PER_MB, grouped[:].bitcast(F32), on_vector)
+            transpose_group(t[:].bitcast(F32), TILES_PER_MB, grouped[:].bitcast(F32),
+                            [mb < 1 or mb % 2 == 1, mb < 1])
             nc.vector.quantize_mx(out=svq[:, cols].bitcast(FP8X4), scales=svs[:, cols], in_=grouped[:])
-            bc = ps_b.tile([P, MB_COLS], F32, name="bc")
-            for j in range(TILES_PER_MB):
-                c = mb * TILES_PER_MB + j
-                nc.tensor.matmul(out=bc[:, j * P:(j + 1) * P],
-                                 lhsT=sv2col[:, c:c + 1].to_broadcast([P, P]),
-                                 rhs=half_ident[:], start=True, stop=True)
-            nc.scalar.copy(out=hsv2b[:, cols], in_=bc[:])
-            if mb + 2 < N_MB:
-                load_sv(mb + 2)
+            if mb + 3 < N_MB:
+                load_sv(mb + 3)
 
-        def main_step(g, nb):
-            mbs = GROUPS[g]
-            width = len(mbs) * MB_COLS
-            w = work.tile([P, 4 * MB_COLS], F32, name="w")
-            for i, mb in enumerate(mbs):
-                cols = slice(mb * MB_COLS, (mb + 1) * MB_COLS)
-                ps = ps_mm.tile([P, MB_COLS], F32, name="ps")
-                nc.tensor.matmul_mx(
-                    out=ps[:],
-                    lhsT=xq[:, nb * P:(nb + 1) * P].bitcast(FP8X4),
-                    lhsT_scale=xs[:, nb * P:(nb + 1) * P],
-                    rhs=svq[:, cols].bitcast(FP8X4),
-                    rhs_scale=svs[:, cols],
-                    start=True, stop=True,
-                )
-                nc.vector.scalar_tensor_tensor(
-                    out=w[:, i * MB_COLS:(i + 1) * MB_COLS], in0=ps[:], scalar=hx2[:, nb:nb + 1],
-                    in1=hsv2b[:, cols], op0=ALU.subtract, op1=ALU.subtract)
-            nc.gpsimd.tensor_scalar(out=w[:, :width], in0=w[:, :width], scalar1=0.0, scalar2=-3.0e38,
-                                    op0=ALU.min, op1=ALU.max)
-            nc.scalar.activation(out=w[:, :width], in_=w[:, :width], func=ACT.Exp, scale=g2[:, 0:1])
-            c0 = mbs[0] * MB_COLS
-            k = nb * n_groups + g
-            nc.vector.scalar_tensor_tensor(
-                out=w[:, :width], in0=w[:, :width], scalar=1.0, in1=dcb[:, c0:c0 + width],
-                op0=ALU.mult, op1=ALU.mult, accum_out=acc[:, k:k + 1])
+        w_tiles = {}
 
-        prep_x_norm(0)
-        prep_sv(0, True)
-        for j in range(1, NB):
-            prep_x_norm(j)
+        def front(i):
+            w = work.tile([P, SVT_PER_W * N_ROWS], F32, name="w")
+            w_tiles[i] = w
+            for s in range(SVT_PER_W):
+                t = i * SVT_PER_W + s
+                for h in range(N_ROWS // HALF):
+                    ps = ps_mm.tile([P, HALF], F32, name="ps")
+                    nc.tensor.matmul_mx(
+                        out=ps[:],
+                        lhsT=svq[:, t * P:(t + 1) * P].bitcast(FP8X4),
+                        lhsT_scale=svs[:, t * P:(t + 1) * P],
+                        rhs=xq[:, h * HALF:(h + 1) * HALF].bitcast(FP8X4),
+                        rhs_scale=xs[:, h * HALF:(h + 1) * HALF],
+                        start=True, stop=True,
+                    )
+                    o = s * N_ROWS + h * HALF
+                    nc.vector.scalar_tensor_tensor(
+                        out=w[:, o:o + HALF], in0=ps[:], scalar=hsv2col[:, t:t + 1],
+                        in1=hx2b[:, h * HALF:(h + 1) * HALF], op0=ALU.subtract, op1=ALU.subtract)
+            nc.scalar.activation(out=w[:], in_=w[:], func=ACT.Exp, scale=g2[:, 0:1])
 
-        for g in range(n_groups):
-            nxt = GROUPS[g + 1] if g + 1 < n_groups else []
-            when = {}
-            for i, mb in enumerate(nxt):
-                when[(i * NB) // len(nxt)] = when.get((i * NB) // len(nxt), []) + [mb]
-            for nb in range(NB):
-                for mb in when.get(nb, []):
-                    prep_sv(mb, False)
-                main_step(g, nb)
+        def weigh(i):
+            w = w_tiles[i]
+            for s in range(SVT_PER_W):
+                t = i * SVT_PER_W + s
+                nc.vector.tensor_scalar(
+                    out=w[:, s * N_ROWS:(s + 1) * N_ROWS], in0=w[:, s * N_ROWS:(s + 1) * N_ROWS],
+                    scalar1=1.0, scalar2=dccol[:, t:t + 1], op0=ALU.min, op1=ALU.mult)
+
+        def back(i):
+            w = w_tiles[i]
+            per_bank = HALF // P
+            for s in range(SVT_PER_W):
+                t = i * SVT_PER_W + s
+                for j in range(NB):
+                    o = s * N_ROWS + j * P
+                    nc.tensor.matmul(out=acc[j // per_bank][:, j % per_bank, :], lhsT=w[:, o:o + P],
+                                     rhs=ident[:], is_transpose=True,
+                                     start=(t == 0 and j % per_bank == 0),
+                                     stop=(t == N_SVT - 1 and j % per_bank == per_bank - 1))
+
+        prep_sv(0)
+        prep_sv(1)
+        w_per_mb = TILES_PER_MB // SVT_PER_W
+        for i in range(N_W + LAG):
+            if i < N_W:
+                if i % w_per_mb == 0 and i // w_per_mb + 2 < N_MB:
+                    prep_sv(i // w_per_mb + 2)
+                front(i)
+            if 1 <= i < N_W + 1:
+                weigh(i - 1)
+            if i >= LAG:
+                back(i - LAG)
 
         res = const.tile([P, NB], F32)
-        nc.vector.tensor_reduce(out=res[:], in_=acc[:].rearrange("p (j g) -> p j g", g=n_groups),
-                                axis=AX.X, op=ALU.add)
+        for h in range(N_ROWS // HALF):
+            nc.vector.tensor_reduce(out=res[:, h * (HALF // P):(h + 1) * (HALF // P)], in_=acc[h][:],
+                                    axis=AX.X, op=ALU.add)
         res2 = const.tile([P, NB], F32)
         nc.vector.tensor_scalar(out=res2[:], in0=res[:], scalar1=ic_f[:, 0:1], scalar2=None, op0=ALU.add)
         nc.sync.dma_start(out=out.rearrange("(p j) -> p j", j=NB), in_=res2[:])

@@ -19,15 +19,21 @@ D = 512
 WORDS = D // 2
 NB = N_ROWS // P
 HALF = 512
+N_HALF = N_ROWS // HALF
+JB = HALF // P
 MB_COLS = 512
 N_MB = M_ROWS // MB_COLS
 TILES_PER_MB = MB_COLS // P
 N_SVT = M_ROWS // P
-SVT_PER_W = 2
-N_W = N_SVT // SVT_PER_W
-LAG = 2
+N_PAIR = N_SVT // 2
+W_LIST = [[2 * i, 2 * i + 1] for i in range(N_PAIR - 1)] + [[N_SVT - 2], [N_SVT - 1]]
+N_W = len(W_LIST)
 
 FLOPS = 2 * N_ROWS * M_ROWS * D
+
+
+def copy_on_vector(q):
+    return q < 3 or q % 3 == 0
 
 
 def tile_rbf_svm_kernel(tc, X, SV, DC, IC, gamma, out):
@@ -35,26 +41,14 @@ def tile_rbf_svm_kernel(tc, X, SV, DC, IC, gamma, out):
     with ExitStack() as ctx:
         const = ctx.enter_context(tc.tile_pool(name="const", bufs=1))
         keep = ctx.enter_context(tc.tile_pool(name="keep", bufs=1))
-        svload = ctx.enter_context(tc.tile_pool(name="svload", bufs=4))
+        svload = ctx.enter_context(tc.tile_pool(name="svload", bufs=5))
         stage = ctx.enter_context(tc.tile_pool(name="stage", bufs=3))
-        work = ctx.enter_context(tc.tile_pool(name="work", bufs=6))
+        work = ctx.enter_context(tc.tile_pool(name="work", bufs=5))
         junkp = ctx.enter_context(tc.tile_pool(name="junkp", bufs=2))
         ps_mm = ctx.enter_context(tc.psum_pool(name="ps_mm", bufs=4))
         ps_t = ctx.enter_context(tc.psum_pool(name="ps_t", bufs=2))
         ps_r = ctx.enter_context(tc.psum_pool(name="ps_r", bufs=1))
-
-        x_nat = keep.tile([P, NB * D], BF16)
-        nc.sync.dma_start(
-            out=x_nat[:].rearrange("p (j d) -> p j d", j=NB),
-            in_=X.rearrange("(p j) d -> p j d", j=NB),
-        )
-        g_bf = const.tile([P, 1], BF16)
-        nc.scalar.dma_start(out=g_bf[:], in_=gamma.partition_broadcast(P))
-        ic_bf = const.tile([P, 1], BF16)
-        nc.scalar.dma_start(out=ic_bf[:], in_=IC.partition_broadcast(P))
-        dc_rows = const.tile([P, P], BF16)
-        nc.vector.memset(dc_rows[:], 0.0)
-        nc.scalar.dma_start(out=dc_rows[0:N_SVT, :], in_=DC.rearrange("o (t p) -> (o t) p", p=P))
+        ctx.enter_context(tc.manual_schedule())
 
         sv_nat = {}
 
@@ -66,104 +60,135 @@ def tile_rbf_svm_kernel(tc, X, SV, DC, IC, gamma, out):
             )
             sv_nat[mb] = t
 
+        x_view = X.rearrange("(p j) d -> p j d", j=NB)
+        x_nat = [keep.tile([P, JB * D], BF16, name="x_nat%d" % h) for h in range(N_HALF)]
+
+        def load_x(h):
+            nc.sync.dma_start(out=x_nat[h][:].rearrange("p (j d) -> p j d", j=JB),
+                              in_=x_view[:, h * JB:(h + 1) * JB, :])
+
+        load_x(0)
         load_sv(0)
+        load_x(1)
         load_sv(1)
         load_sv(2)
+        load_sv(3)
 
+        dc_rows = const.tile([P, P], BF16)
+        nc.vector.memset(dc_rows[:], 0.0)
         warm = const.tile([P, 1], F32)
         nc.vector.memset(warm[:], 0.0)
+        g_bf = const.tile([P, 1], BF16)
+        nc.scalar.dma_start(out=g_bf[:], in_=gamma.partition_broadcast(P))
+        ic_bf = const.tile([P, 1], BF16)
+        nc.scalar.dma_start(out=ic_bf[:], in_=IC.partition_broadcast(P))
+        nc.scalar.dma_start(out=dc_rows[0:N_SVT, :], in_=DC.rearrange("o (t p) -> (o t) p", p=P))
         nc.scalar.activation(out=warm[:], in_=warm[:], func=ACT.Exp)
+
         ident = const.tile([P, P], F32)
         make_identity(nc, ident[:])
         ident_bf = const.tile([P, P], BF16)
         nc.vector.tensor_copy(out=ident_bf[:], in_=ident[:])
         half_ident = const.tile([P, P], F32)
         nc.vector.tensor_scalar(out=half_ident[:], in0=ident[:], scalar1=0.5, scalar2=None, op0=ALU.mult)
-        g2 = const.tile([P, 1], F32)
-        nc.vector.tensor_scalar(out=g2[:], in0=g_bf[:], scalar1=2.0, scalar2=None, op0=ALU.mult)
-        ic_f = const.tile([P, 1], F32)
-        nc.vector.tensor_copy(out=ic_f[:], in_=ic_bf[:])
 
         x2col = keep.tile([P, NB], F32)
         hx2b = keep.tile([P, N_ROWS], F32)
         sv2col = keep.tile([P, N_SVT], F32)
         hsv2col = keep.tile([P, N_SVT], F32)
         dccol = keep.tile([P, N_SVT], F32)
+        g2 = const.tile([P, 1], F32)
+        ic_f = const.tile([P, 1], F32)
 
         xq = keep.tile([P, N_ROWS], U32, align_bytes=64)
         xs = keep.tile([P, N_ROWS], U8, align_bytes=64)
         svq = keep.tile([P, M_ROWS], U32, align_bytes=64)
         svs = keep.tile([P, M_ROWS], U8, align_bytes=64)
+        acc = [ps_r.tile([P, JB, P], F32, name="acc%d" % h) for h in range(N_HALF)]
 
-        acc = [ps_r.tile([P, HALF // P, P], F32, name="acc%d" % h) for h in range(N_ROWS // HALF)]
+        def transpose_pair(src_f32, first_tile):
+            xt = ps_t.tile([P, 4, P], F32, name="xt")
+            for jj in range(2):
+                for u in range(2):
+                    c0 = (first_tile + jj) * WORDS + u * P
+                    nc.tensor.transpose(xt[:, 2 * jj + u, :], src_f32[:, c0:c0 + P], ident[:])
+            return xt
 
-        def transpose_group(src_f32, n_tiles, grouped_f32, on_vector):
-            for pair in range(n_tiles // 2):
-                xt = ps_t.tile([P, 4, P], F32, name="xt")
-                for jj in range(2):
-                    for u in range(2):
-                        c0 = (2 * pair + jj) * WORDS + u * P
-                        nc.tensor.transpose(xt[:, 2 * jj + u, :], src_f32[:, c0:c0 + P], ident[:])
-                dst = grouped_f32[:, pair * 512:(pair + 1) * 512].rearrange(
-                    "p (j r u) -> p j r u", j=2, u=2)
-                src = xt[:].rearrange("p (j u) r -> p j r u", j=2)
-                if on_vector[pair]:
-                    nc.vector.tensor_copy(out=dst, in_=src)
-                else:
-                    nc.scalar.copy(out=dst, in_=src)
+        def copy_pair(xt, dst_f32, on_vector):
+            dst = dst_f32.rearrange("p (j r u) -> p j r u", j=2, u=2)
+            src = xt[:].rearrange("p (j u) r -> p j r u", j=2)
+            if on_vector:
+                nc.vector.tensor_copy(out=dst, in_=src)
+            else:
+                nc.scalar.copy(out=dst, in_=src)
 
         def square_sum(src, col):
             junk = junkp.tile([P, D], BF16, name="junk")
             nc.scalar.activation(out=junk[:], in_=src, func=ACT.Square, accum_out=col)
 
-        for j in range(NB // 2):
-            square_sum(x_nat[:, j * D:(j + 1) * D], x2col[:, j:j + 1])
         gx = keep.tile([P, N_ROWS * 4], BF16, align_bytes=64)
-        transpose_group(x_nat[:].bitcast(F32), NB, gx[:].bitcast(F32), [True] * (NB // 2))
-        nc.vector.quantize_mx(out=xq[:].bitcast(FP8X4), scales=xs[:], in_=gx[:])
-        x2col_v = keep.tile([P, NB], F32)
-        for j in range(NB // 2, NB):
-            junk = junkp.tile([P, D], F32, name="junk_v")
-            nc.vector.scalar_tensor_tensor(
-                out=junk[:], in0=x_nat[:, j * D:(j + 1) * D], scalar=1.0, in1=x_nat[:, j * D:(j + 1) * D],
-                op0=ALU.mult, op1=ALU.mult, accum_out=x2col_v[:, j:j + 1])
-        for h in range(N_ROWS // HALF):
-            bc = ps_t.tile([P, HALF], F32, name="xt")
-            for jj in range(HALF // P):
-                j = h * (HALF // P) + jj
-                nc.tensor.matmul(out=bc[:, jj * P:(jj + 1) * P],
-                                 lhsT=(x2col if h == 0 else x2col_v)[:, j:j + 1].to_broadcast([P, P]),
-                                 rhs=half_ident[:], start=True, stop=True)
-            nc.vector.tensor_copy(out=hx2b[:, h * HALF:(h + 1) * HALF], in_=bc[:])
-
+        gx_f32 = gx[:].bitcast(F32)
+        for h in range(N_HALF):
+            for jj in range(JB):
+                j = h * JB + jj
+                square_sum(x_nat[h][:, jj * D:(jj + 1) * D], x2col[:, j:j + 1])
+        for h in range(N_HALF):
+            for pr in range(JB // 2):
+                xt = transpose_pair(x_nat[h][:].bitcast(F32), 2 * pr)
+                k = h * (JB // 2) + pr
+                copy_pair(xt, gx_f32[:, k * 512:(k + 1) * 512], True)
+            nc.vector.quantize_mx(out=xq[:, h * HALF:(h + 1) * HALF].bitcast(FP8X4),
+                                  scales=xs[:, h * HALF:(h + 1) * HALF],
+                                  in_=gx[:, h * HALF * 4:(h + 1) * HALF * 4])
         dct = ps_t.tile([P, P], BF16, name="xt")
         nc.tensor.transpose(dct[:], dc_rows[:], ident_bf[:])
         nc.vector.tensor_copy(out=dccol[:], in_=dct[:, 0:N_SVT])
+        nc.vector.tensor_scalar(out=g2[:], in0=g_bf[:], scalar1=2.0, scalar2=None, op0=ALU.mult)
+        nc.vector.tensor_copy(out=ic_f[:], in_=ic_bf[:])
 
-        def prep_sv(mb):
-            t = sv_nat[mb]
-            cols = slice(mb * MB_COLS, (mb + 1) * MB_COLS)
-            c0 = mb * TILES_PER_MB
-            for j in range(TILES_PER_MB):
-                square_sum(t[:, j * D:(j + 1) * D], sv2col[:, c0 + j:c0 + j + 1])
-            nc.vector.tensor_scalar(out=hsv2col[:, c0:c0 + TILES_PER_MB], in0=sv2col[:, c0:c0 + TILES_PER_MB],
-                                    scalar1=0.5, scalar2=None, op0=ALU.mult)
-            grouped = stage.tile([P, MB_COLS * 4], BF16, align_bytes=64, name="grouped")
-            transpose_group(t[:].bitcast(F32), TILES_PER_MB, grouped[:].bitcast(F32),
-                            [mb < 1 or mb % 2 == 1, mb < 1])
-            nc.vector.quantize_mx(out=svq[:, cols].bitcast(FP8X4), scales=svs[:, cols], in_=grouped[:])
-            if mb + 3 < N_MB:
-                load_sv(mb + 3)
+        def spread_x_norms():
+            for h in range(N_HALF):
+                bc = ps_mm.tile([P, HALF], F32, name="ps")
+                for jj in range(JB):
+                    j = h * JB + jj
+                    nc.tensor.matmul(out=bc[:, jj * P:(jj + 1) * P],
+                                     lhsT=x2col[:, j:j + 1].to_broadcast([P, P]),
+                                     rhs=half_ident[:], start=True, stop=True)
+                nc.vector.tensor_copy(out=hx2b[:, h * HALF:(h + 1) * HALF], in_=bc[:])
 
-        w_tiles = {}
+        xt_of = {}
+        grouped_of = {}
+        ps_of = {}
+        w_of = {}
 
-        def front(i):
-            w = work.tile([P, SVT_PER_W * N_ROWS], F32, name="w")
-            w_tiles[i] = w
-            for s in range(SVT_PER_W):
-                t = i * SVT_PER_W + s
-                for h in range(N_ROWS // HALF):
+        def pair_src(q):
+            return sv_nat[q // 2], (q % 2) * 2
+
+        def in_transposes(q):
+            t, first = pair_src(q)
+            xt_of[q] = transpose_pair(t[:].bitcast(F32), first)
+
+        def squares(q):
+            t, first = pair_src(q)
+            for jj in range(2):
+                square_sum(t[:, (first + jj) * D:(first + jj + 1) * D], sv2col[:, 2 * q + jj:2 * q + jj + 1])
+            nc.gpsimd.tensor_scalar(out=hsv2col[:, 2 * q:2 * q + 2], in0=sv2col[:, 2 * q:2 * q + 2],
+                                    scalar1=0.5, scalar2=0.0, op0=ALU.mult, op1=ALU.add)
+
+        def copy_out(q):
+            grouped = stage.tile([P, 2 * P * 4], BF16, align_bytes=64, name="grouped")
+            grouped_of[q] = grouped
+            copy_pair(xt_of[q], grouped[:].bitcast(F32), copy_on_vector(q))
+
+        def quantise(q):
+            cols = slice(q * 2 * P, (q + 1) * 2 * P)
+            nc.vector.quantize_mx(out=svq[:, cols].bitcast(FP8X4), scales=svs[:, cols], in_=grouped_of[q][:])
+
+        def cross(i):
+            for s, t in enumerate(W_LIST[i]):
+                for h in range(N_HALF):
                     ps = ps_mm.tile([P, HALF], F32, name="ps")
+                    ps_of[(i, s, h)] = ps
                     nc.tensor.matmul_mx(
                         out=ps[:],
                         lhsT=svq[:, t * P:(t + 1) * P].bitcast(FP8X4),
@@ -172,49 +197,71 @@ def tile_rbf_svm_kernel(tc, X, SV, DC, IC, gamma, out):
                         rhs_scale=xs[:, h * HALF:(h + 1) * HALF],
                         start=True, stop=True,
                     )
+
+        def distances(i):
+            w = work.tile([P, 2 * N_ROWS], F32, name="w")
+            w_of[i] = w
+            for s, t in enumerate(W_LIST[i]):
+                for h in range(N_HALF):
                     o = s * N_ROWS + h * HALF
                     nc.vector.scalar_tensor_tensor(
-                        out=w[:, o:o + HALF], in0=ps[:], scalar=hsv2col[:, t:t + 1],
+                        out=w[:, o:o + HALF], in0=ps_of[(i, s, h)][:], scalar=hsv2col[:, t:t + 1],
                         in1=hx2b[:, h * HALF:(h + 1) * HALF], op0=ALU.subtract, op1=ALU.subtract)
-            nc.scalar.activation(out=w[:], in_=w[:], func=ACT.Exp, scale=g2[:, 0:1])
+
+        def exponent(i):
+            width = len(W_LIST[i]) * N_ROWS
+            nc.scalar.activation(out=w_of[i][:, :width], in_=w_of[i][:, :width], func=ACT.Exp,
+                                 scale=g2[:, 0:1])
 
         def weigh(i):
-            w = w_tiles[i]
-            for s in range(SVT_PER_W):
-                t = i * SVT_PER_W + s
+            w = w_of[i]
+            for s, t in enumerate(W_LIST[i]):
                 nc.vector.tensor_scalar(
                     out=w[:, s * N_ROWS:(s + 1) * N_ROWS], in0=w[:, s * N_ROWS:(s + 1) * N_ROWS],
                     scalar1=1.0, scalar2=dccol[:, t:t + 1], op0=ALU.min, op1=ALU.mult)
 
-        def back(i):
-            w = w_tiles[i]
-            per_bank = HALF // P
-            for s in range(SVT_PER_W):
-                t = i * SVT_PER_W + s
+        def add_up(i):
+            w = w_of[i]
+            for s, t in enumerate(W_LIST[i]):
                 for j in range(NB):
                     o = s * N_ROWS + j * P
-                    nc.tensor.matmul(out=acc[j // per_bank][:, j % per_bank, :], lhsT=w[:, o:o + P],
+                    nc.tensor.matmul(out=acc[j // JB][:, j % JB, :], lhsT=w[:, o:o + P],
                                      rhs=ident[:], is_transpose=True,
-                                     start=(t == 0 and j % per_bank == 0),
-                                     stop=(t == N_SVT - 1 and j % per_bank == per_bank - 1))
+                                     start=(t == 0 and j % JB == 0),
+                                     stop=(t == N_SVT - 1 and j % JB == JB - 1))
 
-        prep_sv(0)
-        prep_sv(1)
-        w_per_mb = TILES_PER_MB // SVT_PER_W
-        for i in range(N_W + LAG):
-            if i < N_W:
-                if i % w_per_mb == 0 and i // w_per_mb + 2 < N_MB:
-                    prep_sv(i // w_per_mb + 2)
-                front(i)
-            if 1 <= i < N_W + 1:
+        def period(i):
+            if 0 <= i < N_W:
+                distances(i)
+            if 0 <= i + 3 < N_PAIR:
+                squares(i + 3)
+                if not copy_on_vector(i + 3):
+                    copy_out(i + 3)
+            if 0 <= i < N_W:
+                exponent(i)
+            if 0 <= i - 1 < N_W:
                 weigh(i - 1)
-            if i >= LAG:
-                back(i - LAG)
+            if 0 <= i + 2 < N_PAIR:
+                quantise(i + 2)
+            if 0 <= i + 3 < N_PAIR and copy_on_vector(i + 3):
+                copy_out(i + 3)
+            if 0 <= i - 2 < N_W:
+                add_up(i - 2)
+            if 0 <= i + 4 < N_PAIR:
+                in_transposes(i + 4)
+            if 0 <= i + 1 < N_W:
+                cross(i + 1)
+            if (i + 8) % 2 == 0 and 4 <= (i + 8) // 2 < N_MB:
+                load_sv((i + 8) // 2)
+
+        for i in range(-4, N_W + 2):
+            if i == -1:
+                spread_x_norms()
+            period(i)
 
         res = const.tile([P, NB], F32)
-        for h in range(N_ROWS // HALF):
-            nc.vector.tensor_reduce(out=res[:, h * (HALF // P):(h + 1) * (HALF // P)], in_=acc[h][:],
-                                    axis=AX.X, op=ALU.add)
+        for h in range(N_HALF):
+            nc.vector.tensor_reduce(out=res[:, h * JB:(h + 1) * JB], in_=acc[h][:], axis=AX.X, op=ALU.add)
         res2 = const.tile([P, NB], F32)
         nc.vector.tensor_scalar(out=res2[:], in0=res[:], scalar1=ic_f[:, 0:1], scalar2=None, op0=ALU.add)
         nc.sync.dma_start(out=out.rearrange("(p j) -> p j", j=NB), in_=res2[:])

@@ -184,8 +184,9 @@ def tile_rbf_svm_kernel(tc, X, SV, DC, IC, gamma, out):
             cols = slice(q * 2 * P, (q + 1) * 2 * P)
             nc.vector.quantize_mx(out=svq[:, cols].bitcast(FP8X4), scales=svs[:, cols], in_=grouped_of[q][:])
 
-        def cross(i):
-            for s, t in enumerate(W_LIST[i]):
+        def cross(i, s):
+            if s < len(W_LIST[i]):
+                t = W_LIST[i][s]
                 for h in range(N_HALF):
                     ps = ps_mm.tile([P, HALF], F32, name="ps")
                     ps_of[(i, s, h)] = ps
@@ -220,9 +221,10 @@ def tile_rbf_svm_kernel(tc, X, SV, DC, IC, gamma, out):
                     out=w[:, s * N_ROWS:(s + 1) * N_ROWS], in0=w[:, s * N_ROWS:(s + 1) * N_ROWS],
                     scalar1=1.0, scalar2=dccol[:, t:t + 1], op0=ALU.min, op1=ALU.mult)
 
-        def add_up(i):
+        def add_up(i, s):
             w = w_of[i]
-            for s, t in enumerate(W_LIST[i]):
+            if s < len(W_LIST[i]):
+                t = W_LIST[i][s]
                 for j in range(NB):
                     o = s * N_ROWS + j * P
                     nc.tensor.matmul(out=acc[j // JB][:, j % JB, :], lhsT=w[:, o:o + P],
@@ -245,12 +247,13 @@ def tile_rbf_svm_kernel(tc, X, SV, DC, IC, gamma, out):
                 quantise(i + 2)
             if 0 <= i + 3 < N_PAIR and copy_on_vector(i + 3):
                 copy_out(i + 3)
-            if 0 <= i - 2 < N_W:
-                add_up(i - 2)
-            if 0 <= i + 4 < N_PAIR:
-                in_transposes(i + 4)
-            if 0 <= i + 1 < N_W:
-                cross(i + 1)
+            for s in range(2):
+                if 0 <= i - 2 < N_W:
+                    add_up(i - 2, s)
+                if s == 1 and 0 <= i + 4 < N_PAIR:
+                    in_transposes(i + 4)
+                if 0 <= i + 1 < N_W:
+                    cross(i + 1, s)
             if (i + 8) % 2 == 0 and 4 <= (i + 8) // 2 < N_MB:
                 load_sv((i + 8) // 2)
 

@@ -33,7 +33,7 @@ FLOPS = 2 * N_ROWS * M_ROWS * D
 
 
 def copy_on_vector(q):
-    return q < 3 or q % 3 == 0
+    return q < 2 or q % 5 == 0
 
 
 def tile_rbf_svm_kernel(tc, X, SV, DC, IC, gamma, out):
@@ -41,7 +41,7 @@ def tile_rbf_svm_kernel(tc, X, SV, DC, IC, gamma, out):
     with ExitStack() as ctx:
         const = ctx.enter_context(tc.tile_pool(name="const", bufs=1))
         keep = ctx.enter_context(tc.tile_pool(name="keep", bufs=1))
-        svload = ctx.enter_context(tc.tile_pool(name="svload", bufs=5))
+        svload = ctx.enter_context(tc.tile_pool(name="svload", bufs=6))
         stage = ctx.enter_context(tc.tile_pool(name="stage", bufs=3))
         work = ctx.enter_context(tc.tile_pool(name="work", bufs=5))
         junkp = ctx.enter_context(tc.tile_pool(name="junkp", bufs=2))
@@ -64,12 +64,14 @@ def tile_rbf_svm_kernel(tc, X, SV, DC, IC, gamma, out):
         x_nat = [keep.tile([P, JB * D], BF16, name="x_nat%d" % h) for h in range(N_HALF)]
 
         def load_x(h):
-            nc.sync.dma_start(out=x_nat[h][:].rearrange("p (j d) -> p j d", j=JB),
-                              in_=x_view[:, h * JB:(h + 1) * JB, :])
+            for a in range(2):
+                nc.sync.dma_start(
+                    out=x_nat[h][:, a * 2 * D:(a + 1) * 2 * D].rearrange("p (j d) -> p j d", j=2),
+                    in_=x_view[:, h * JB + 2 * a:h * JB + 2 * a + 2, :])
 
         load_x(0)
-        load_sv(0)
         load_x(1)
+        load_sv(0)
         load_sv(1)
         load_sv(2)
         load_sv(3)
@@ -184,9 +186,8 @@ def tile_rbf_svm_kernel(tc, X, SV, DC, IC, gamma, out):
             cols = slice(q * 2 * P, (q + 1) * 2 * P)
             nc.vector.quantize_mx(out=svq[:, cols].bitcast(FP8X4), scales=svs[:, cols], in_=grouped_of[q][:])
 
-        def cross(i, s):
-            if s < len(W_LIST[i]):
-                t = W_LIST[i][s]
+        def cross(i):
+            for s, t in enumerate(W_LIST[i]):
                 for h in range(N_HALF):
                     ps = ps_mm.tile([P, HALF], F32, name="ps")
                     ps_of[(i, s, h)] = ps
@@ -221,10 +222,9 @@ def tile_rbf_svm_kernel(tc, X, SV, DC, IC, gamma, out):
                     out=w[:, s * N_ROWS:(s + 1) * N_ROWS], in0=w[:, s * N_ROWS:(s + 1) * N_ROWS],
                     scalar1=1.0, scalar2=dccol[:, t:t + 1], op0=ALU.min, op1=ALU.mult)
 
-        def add_up(i, s):
+        def add_up(i):
             w = w_of[i]
-            if s < len(W_LIST[i]):
-                t = W_LIST[i][s]
+            for s, t in enumerate(W_LIST[i]):
                 for j in range(NB):
                     o = s * N_ROWS + j * P
                     nc.tensor.matmul(out=acc[j // JB][:, j % JB, :], lhsT=w[:, o:o + P],
@@ -235,10 +235,10 @@ def tile_rbf_svm_kernel(tc, X, SV, DC, IC, gamma, out):
         def period(i):
             if 0 <= i < N_W:
                 distances(i)
-            if 0 <= i + 3 < N_PAIR:
-                squares(i + 3)
-                if not copy_on_vector(i + 3):
-                    copy_out(i + 3)
+            if 0 <= i + 2 < N_PAIR:
+                squares(i + 2)
+            if 0 <= i + 3 < N_PAIR and not copy_on_vector(i + 3):
+                copy_out(i + 3)
             if 0 <= i < N_W:
                 exponent(i)
             if 0 <= i - 1 < N_W:
@@ -247,13 +247,12 @@ def tile_rbf_svm_kernel(tc, X, SV, DC, IC, gamma, out):
                 quantise(i + 2)
             if 0 <= i + 3 < N_PAIR and copy_on_vector(i + 3):
                 copy_out(i + 3)
-            for s in range(2):
-                if 0 <= i - 2 < N_W:
-                    add_up(i - 2, s)
-                if s == 1 and 0 <= i + 4 < N_PAIR:
-                    in_transposes(i + 4)
-                if 0 <= i + 1 < N_W:
-                    cross(i + 1, s)
+            if 0 <= i - 2 < N_W:
+                add_up(i - 2)
+            if 0 <= i + 4 < N_PAIR:
+                in_transposes(i + 4)
+            if 0 <= i + 1 < N_W:
+                cross(i + 1)
             if (i + 8) % 2 == 0 and 4 <= (i + 8) // 2 < N_MB:
                 load_sv((i + 8) // 2)
 

@@ -26,8 +26,11 @@ N_MB = M_ROWS // MB_COLS
 TILES_PER_MB = MB_COLS // P
 N_SVT = M_ROWS // P
 N_PAIR = N_SVT // 2
-W_LIST = [[2 * i, 2 * i + 1] for i in range(N_PAIR - 1)] + [[N_SVT - 2], [N_SVT - 1]]
-N_W = len(W_LIST)
+UNITS = ([[(0, 0), (1, 0)], [(0, 1), (1, 1)]]
+         + [[(t, h) for t in (2 * q, 2 * q + 1) for h in range(N_HALF)] for q in range(1, N_PAIR - 1)]
+         + [[(N_SVT - 2, 0), (N_SVT - 2, 1)], [(N_SVT - 1, 0)], [(N_SVT - 1, 1)]])
+N_U = len(UNITS)
+FIRST, REST = slice(0, 2), slice(2, None)
 
 FLOPS = 2 * N_ROWS * M_ROWS * D
 
@@ -52,13 +55,14 @@ def tile_rbf_svm_kernel(tc, X, SV, DC, IC, gamma, out):
 
         sv_nat = {}
 
-        def load_sv(mb):
-            t = svload.tile([P, TILES_PER_MB * D], BF16, name="sv_nat")
+        def load_sv(mb, first=0, tiles=TILES_PER_MB):
+            if first == 0:
+                sv_nat[mb] = svload.tile([P, TILES_PER_MB * D], BF16, name="sv_nat")
+            r0 = mb * MB_COLS + first * P
             nc.sync.dma_start(
-                out=t[:].rearrange("p (j d) -> p j d", j=TILES_PER_MB),
-                in_=SV[mb * MB_COLS:(mb + 1) * MB_COLS, :].rearrange("(j p) d -> p j d", p=P),
+                out=sv_nat[mb][:, first * D:(first + tiles) * D].rearrange("p (j d) -> p j d", j=tiles),
+                in_=SV[r0:r0 + tiles * P, :].rearrange("(j p) d -> p j d", p=P),
             )
-            sv_nat[mb] = t
 
         x_view = X.rearrange("(p j) d -> p j d", j=NB)
         x_nat = [keep.tile([P, JB * D], BF16, name="x_nat%d" % h) for h in range(N_HALF)]
@@ -70,8 +74,9 @@ def tile_rbf_svm_kernel(tc, X, SV, DC, IC, gamma, out):
                     in_=x_view[:, h * JB + 2 * a:h * JB + 2 * a + 2, :])
 
         load_x(0)
+        load_sv(0, 0, 2)
         load_x(1)
-        load_sv(0)
+        load_sv(0, 2, 2)
         load_sv(1)
         load_sv(2)
         load_sv(3)
@@ -130,33 +135,44 @@ def tile_rbf_svm_kernel(tc, X, SV, DC, IC, gamma, out):
 
         gx = keep.tile([P, N_ROWS * 4], BF16, align_bytes=64)
         gx_f32 = gx[:].bitcast(F32)
-        for h in range(N_HALF):
+
+        def x_squares(h):
             for jj in range(JB):
                 j = h * JB + jj
                 square_sum(x_nat[h][:, jj * D:(jj + 1) * D], x2col[:, j:j + 1])
-        for h in range(N_HALF):
+
+        xt_x = {}
+
+        def x_transposes(h):
             for pr in range(JB // 2):
-                xt = transpose_pair(x_nat[h][:].bitcast(F32), 2 * pr)
+                xt_x[(h, pr)] = transpose_pair(x_nat[h][:].bitcast(F32), 2 * pr)
+
+        def x_quantise(h):
+            for pr in range(JB // 2):
                 k = h * (JB // 2) + pr
-                copy_pair(xt, gx_f32[:, k * 512:(k + 1) * 512], True)
+                copy_pair(xt_x[(h, pr)], gx_f32[:, k * 512:(k + 1) * 512], True)
             nc.vector.quantize_mx(out=xq[:, h * HALF:(h + 1) * HALF].bitcast(FP8X4),
                                   scales=xs[:, h * HALF:(h + 1) * HALF],
                                   in_=gx[:, h * HALF * 4:(h + 1) * HALF * 4])
-        dct = ps_t.tile([P, P], BF16, name="xt")
-        nc.tensor.transpose(dct[:], dc_rows[:], ident_bf[:])
-        nc.vector.tensor_copy(out=dccol[:], in_=dct[:, 0:N_SVT])
-        nc.vector.tensor_scalar(out=g2[:], in0=g_bf[:], scalar1=2.0, scalar2=None, op0=ALU.mult)
-        nc.vector.tensor_copy(out=ic_f[:], in_=ic_bf[:])
 
-        def spread_x_norms():
-            for h in range(N_HALF):
-                bc = ps_mm.tile([P, HALF], F32, name="ps")
-                for jj in range(JB):
-                    j = h * JB + jj
-                    nc.tensor.matmul(out=bc[:, jj * P:(jj + 1) * P],
-                                     lhsT=x2col[:, j:j + 1].to_broadcast([P, P]),
-                                     rhs=half_ident[:], start=True, stop=True)
-                nc.vector.tensor_copy(out=hx2b[:, h * HALF:(h + 1) * HALF], in_=bc[:])
+        bc_of = {}
+
+        def spread_x_norms(h):
+            bc_of[h] = ps_mm.tile([P, HALF], F32, name="ps")
+            for jj in range(JB):
+                j = h * JB + jj
+                nc.tensor.matmul(out=bc_of[h][:, jj * P:(jj + 1) * P],
+                                 lhsT=x2col[:, j:j + 1].to_broadcast([P, P]),
+                                 rhs=half_ident[:], start=True, stop=True)
+
+        def keep_x_norms(h):
+            nc.vector.tensor_copy(out=hx2b[:, h * HALF:(h + 1) * HALF], in_=bc_of[h][:])
+
+        def dc_to_columns():
+            dct = ps_t.tile([P, P], BF16, name="xt")
+            nc.tensor.transpose(dct[:], dc_rows[:], ident_bf[:])
+            nc.vector.tensor_copy(out=dccol[:], in_=dct[:, 0:N_SVT])
+            nc.vector.tensor_copy(out=ic_f[:], in_=ic_bf[:])
 
         xt_of = {}
         grouped_of = {}
@@ -186,80 +202,118 @@ def tile_rbf_svm_kernel(tc, X, SV, DC, IC, gamma, out):
             cols = slice(q * 2 * P, (q + 1) * 2 * P)
             nc.vector.quantize_mx(out=svq[:, cols].bitcast(FP8X4), scales=svs[:, cols], in_=grouped_of[q][:])
 
-        def cross(i):
-            for s, t in enumerate(W_LIST[i]):
-                for h in range(N_HALF):
-                    ps = ps_mm.tile([P, HALF], F32, name="ps")
-                    ps_of[(i, s, h)] = ps
-                    nc.tensor.matmul_mx(
-                        out=ps[:],
-                        lhsT=svq[:, t * P:(t + 1) * P].bitcast(FP8X4),
-                        lhsT_scale=svs[:, t * P:(t + 1) * P],
-                        rhs=xq[:, h * HALF:(h + 1) * HALF].bitcast(FP8X4),
-                        rhs_scale=xs[:, h * HALF:(h + 1) * HALF],
-                        start=True, stop=True,
-                    )
+        def cross(u, part=slice(None)):
+            for t, h in UNITS[u][part]:
+                ps = ps_mm.tile([P, HALF], F32, name="ps")
+                ps_of[(t, h)] = ps
+                nc.tensor.matmul_mx(
+                    out=ps[:],
+                    lhsT=svq[:, t * P:(t + 1) * P].bitcast(FP8X4),
+                    lhsT_scale=svs[:, t * P:(t + 1) * P],
+                    rhs=xq[:, h * HALF:(h + 1) * HALF].bitcast(FP8X4),
+                    rhs_scale=xs[:, h * HALF:(h + 1) * HALF],
+                    start=True, stop=True,
+                )
 
-        def distances(i):
+        def distances(u):
             w = work.tile([P, 2 * N_ROWS], F32, name="w")
-            w_of[i] = w
-            for s, t in enumerate(W_LIST[i]):
-                for h in range(N_HALF):
-                    o = s * N_ROWS + h * HALF
-                    nc.vector.scalar_tensor_tensor(
-                        out=w[:, o:o + HALF], in0=ps_of[(i, s, h)][:], scalar=hsv2col[:, t:t + 1],
-                        in1=hx2b[:, h * HALF:(h + 1) * HALF], op0=ALU.subtract, op1=ALU.subtract)
+            w_of[u] = w
+            for k, (t, h) in enumerate(UNITS[u]):
+                nc.vector.scalar_tensor_tensor(
+                    out=w[:, k * HALF:(k + 1) * HALF], in0=ps_of[(t, h)][:], scalar=hsv2col[:, t:t + 1],
+                    in1=hx2b[:, h * HALF:(h + 1) * HALF], op0=ALU.subtract, op1=ALU.subtract)
 
-        def exponent(i):
-            width = len(W_LIST[i]) * N_ROWS
-            nc.scalar.activation(out=w_of[i][:, :width], in_=w_of[i][:, :width], func=ACT.Exp,
+        def exponent(u):
+            width = len(UNITS[u]) * HALF
+            nc.scalar.activation(out=w_of[u][:, :width], in_=w_of[u][:, :width], func=ACT.Exp,
                                  scale=g2[:, 0:1])
 
-        def weigh(i):
-            w = w_of[i]
-            for s, t in enumerate(W_LIST[i]):
+        def weigh(u):
+            w = w_of[u]
+            k = 0
+            while k < len(UNITS[u]):
+                t = UNITS[u][k][0]
+                e = k + 1
+                while e < len(UNITS[u]) and UNITS[u][e][0] == t:
+                    e += 1
                 nc.vector.tensor_scalar(
-                    out=w[:, s * N_ROWS:(s + 1) * N_ROWS], in0=w[:, s * N_ROWS:(s + 1) * N_ROWS],
+                    out=w[:, k * HALF:e * HALF], in0=w[:, k * HALF:e * HALF],
                     scalar1=1.0, scalar2=dccol[:, t:t + 1], op0=ALU.min, op1=ALU.mult)
+                k = e
 
-        def add_up(i):
-            w = w_of[i]
-            for s, t in enumerate(W_LIST[i]):
-                for j in range(NB):
-                    o = s * N_ROWS + j * P
-                    nc.tensor.matmul(out=acc[j // JB][:, j % JB, :], lhsT=w[:, o:o + P],
+        def add_up(u, part=slice(None)):
+            w = w_of[u]
+            for k, (t, h) in list(enumerate(UNITS[u]))[part]:
+                for jj in range(JB):
+                    o = k * HALF + jj * P
+                    nc.tensor.matmul(out=acc[h][:, jj, :], lhsT=w[:, o:o + P],
                                      rhs=ident[:], is_transpose=True,
-                                     start=(t == 0 and j % JB == 0),
-                                     stop=(t == N_SVT - 1 and j % JB == JB - 1))
+                                     start=(t == 0 and jj == 0),
+                                     stop=(t == N_SVT - 1 and jj == JB - 1))
 
-        def period(i):
-            if 0 <= i < N_W:
-                distances(i)
-            if 0 <= i + 2 < N_PAIR:
-                squares(i + 2)
-            if 0 <= i + 3 < N_PAIR and not copy_on_vector(i + 3):
-                copy_out(i + 3)
-            if 0 <= i < N_W:
-                exponent(i)
-            if 0 <= i - 1 < N_W:
-                weigh(i - 1)
-            if 0 <= i + 2 < N_PAIR:
-                quantise(i + 2)
-            if 0 <= i + 3 < N_PAIR and copy_on_vector(i + 3):
-                copy_out(i + 3)
-            if 0 <= i - 2 < N_W:
-                add_up(i - 2)
-            if 0 <= i + 4 < N_PAIR:
-                in_transposes(i + 4)
-            if 0 <= i + 1 < N_W:
-                cross(i + 1)
-            if (i + 8) % 2 == 0 and 4 <= (i + 8) // 2 < N_MB:
-                load_sv((i + 8) // 2)
+        x_squares(0)
+        x_transposes(0)
+        x_quantise(0)
+        nc.vector.tensor_scalar(out=g2[:], in0=g_bf[:], scalar1=2.0, scalar2=None, op0=ALU.mult)
+        in_transposes(0)
+        squares(0)
+        spread_x_norms(0)
+        copy_out(0)
+        x_transposes(1)
+        quantise(0)
+        keep_x_norms(0)
+        cross(0)
+        x_squares(1)
+        distances(0)
+        spread_x_norms(1)
+        x_quantise(1)
+        in_transposes(1)
+        exponent(0)
+        copy_out(1)
+        dc_to_columns()
+        squares(1)
+        keep_x_norms(1)
+        in_transposes(2)
+        quantise(1)
+        copy_out(2)
+        cross(1)
+        distances(1)
+        exponent(1)
+        weigh(0)
+        in_transposes(3)
+        squares(2)
+        cross(2)
+        quantise(2)
+        copy_out(3)
+        in_transposes(4)
+        load_sv(4)
 
-        for i in range(-4, N_W + 2):
-            if i == -1:
-                spread_x_norms()
-            period(i)
+        for u in range(2, N_U + 2):
+            q = u - 1
+            if u < N_U:
+                distances(u)
+            if q + 2 < N_PAIR:
+                squares(q + 2)
+            if q + 3 < N_PAIR and not copy_on_vector(q + 3):
+                copy_out(q + 3)
+            if u < N_U:
+                exponent(u)
+            if u - 1 < N_U:
+                weigh(u - 1)
+            if q + 2 < N_PAIR:
+                quantise(q + 2)
+            if q + 3 < N_PAIR and copy_on_vector(q + 3):
+                copy_out(q + 3)
+            add_up(u - 2, FIRST)
+            if u + 1 < N_U:
+                cross(u + 1, FIRST)
+            add_up(u - 2, REST)
+            if q + 4 < N_PAIR:
+                in_transposes(q + 4)
+            if u + 1 < N_U:
+                cross(u + 1, REST)
+            if q % 2 == 0 and 5 <= q // 2 + 4 < N_MB:
+                load_sv(q // 2 + 4)
 
         res = const.tile([P, NB], F32)
         for h in range(N_HALF):

@@ -1,3 +1,4 @@
+import math
 from contextlib import ExitStack
 
 import concourse.mybir as mybir
@@ -32,11 +33,15 @@ UNITS = ([[(0, 0), (1, 0)], [(0, 1), (1, 1)]]
 N_U = len(UNITS)
 FIRST, REST = slice(0, 2), slice(2, None)
 
+
+def by_gram(q):
+    return 4 <= q < N_PAIR - 1 and q % 2 == 0
+
 FLOPS = 2 * N_ROWS * M_ROWS * D
 
 
 def copy_on_vector(q):
-    return q < 2 or q % 5 == 0
+    return q < 2
 
 
 def tile_rbf_svm_kernel(tc, X, SV, DC, IC, gamma, out):
@@ -45,7 +50,7 @@ def tile_rbf_svm_kernel(tc, X, SV, DC, IC, gamma, out):
         const = ctx.enter_context(tc.tile_pool(name="const", bufs=1))
         keep = ctx.enter_context(tc.tile_pool(name="keep", bufs=1))
         svload = ctx.enter_context(tc.tile_pool(name="svload", bufs=6))
-        stage = ctx.enter_context(tc.tile_pool(name="stage", bufs=3))
+        stage = ctx.enter_context(tc.tile_pool(name="stage", bufs=4))
         work = ctx.enter_context(tc.tile_pool(name="work", bufs=5))
         junkp = ctx.enter_context(tc.tile_pool(name="junkp", bufs=2))
         ps_mm = ctx.enter_context(tc.psum_pool(name="ps_mm", bufs=4))
@@ -101,8 +106,8 @@ def tile_rbf_svm_kernel(tc, X, SV, DC, IC, gamma, out):
 
         x2col = keep.tile([P, NB], F32)
         hx2b = keep.tile([P, N_ROWS], F32)
-        sv2col = keep.tile([P, N_SVT], F32)
         hsv2col = keep.tile([P, N_SVT], F32)
+        minus_hsv2 = keep.tile([P, N_PAIR], F32)
         dccol = keep.tile([P, N_SVT], F32)
         g2 = const.tile([P, 1], F32)
         ic_f = const.tile([P, 1], F32)
@@ -129,9 +134,9 @@ def tile_rbf_svm_kernel(tc, X, SV, DC, IC, gamma, out):
             else:
                 nc.scalar.copy(out=dst, in_=src)
 
-        def square_sum(src, col):
+        def square_sum(src, col, scale):
             junk = junkp.tile([P, D], BF16, name="junk")
-            nc.scalar.activation(out=junk[:], in_=src, func=ACT.Square, accum_out=col)
+            nc.scalar.activation(out=junk[:], in_=src, func=ACT.Square, scale=scale, accum_out=col)
 
         gx = keep.tile([P, N_ROWS * 4], BF16, align_bytes=64)
         gx_f32 = gx[:].bitcast(F32)
@@ -139,7 +144,7 @@ def tile_rbf_svm_kernel(tc, X, SV, DC, IC, gamma, out):
         def x_squares(h):
             for jj in range(JB):
                 j = h * JB + jj
-                square_sum(x_nat[h][:, jj * D:(jj + 1) * D], x2col[:, j:j + 1])
+                square_sum(x_nat[h][:, jj * D:(jj + 1) * D], x2col[:, j:j + 1], 1.0)
 
         xt_x = {}
 
@@ -188,10 +193,25 @@ def tile_rbf_svm_kernel(tc, X, SV, DC, IC, gamma, out):
 
         def squares(q):
             t, first = pair_src(q)
-            for jj in range(2):
-                square_sum(t[:, (first + jj) * D:(first + jj + 1) * D], sv2col[:, 2 * q + jj:2 * q + jj + 1])
-            nc.gpsimd.tensor_scalar(out=hsv2col[:, 2 * q:2 * q + 2], in0=sv2col[:, 2 * q:2 * q + 2],
-                                    scalar1=0.5, scalar2=0.0, op0=ALU.mult, op1=ALU.add)
+            for jj in range(1 if by_gram(q) else 0, 2):
+                square_sum(t[:, (first + jj) * D:(first + jj + 1) * D],
+                           hsv2col[:, 2 * q + jj:2 * q + jj + 1], math.sqrt(0.5))
+
+        gram_of = {}
+
+        def gram(q):
+            g = ps_mm.tile([P, HALF], F32, name="ps")
+            gram_of[q] = g
+            rows = grouped_of[q][:].rearrange("p (r e) -> p r e", e=4)
+            for e in range(4):
+                side = rows[:, 0:P, e]
+                nc.tensor.matmul(out=g[:, 0:P], lhsT=side, rhs=side, start=(e == 0), stop=(e == 3))
+
+        def diagonal(q):
+            junk = junkp.tile([P, P], F32, name="junk_g")
+            nc.vector.scalar_tensor_tensor(out=junk[:], in0=gram_of[q][:, 0:P], scalar=-0.5, in1=ident[:],
+                                           op0=ALU.mult, op1=ALU.mult,
+                                           accum_out=minus_hsv2[:, q:q + 1])
 
         def copy_out(q):
             grouped = stage.tile([P, 2 * P * 4], BF16, align_bytes=64, name="grouped")
@@ -215,13 +235,18 @@ def tile_rbf_svm_kernel(tc, X, SV, DC, IC, gamma, out):
                     start=True, stop=True,
                 )
 
-        def distances(u):
-            w = work.tile([P, 2 * N_ROWS], F32, name="w")
-            w_of[u] = w
-            for k, (t, h) in enumerate(UNITS[u]):
+        def distances(u, part=slice(None)):
+            if u not in w_of:
+                w_of[u] = work.tile([P, 2 * N_ROWS], F32, name="w")
+            w = w_of[u]
+            for k, (t, h) in list(enumerate(UNITS[u]))[part]:
+                if t % 2 == 0 and by_gram(t // 2):
+                    norm, op = minus_hsv2[:, t // 2:t // 2 + 1], ALU.add
+                else:
+                    norm, op = hsv2col[:, t:t + 1], ALU.subtract
                 nc.vector.scalar_tensor_tensor(
-                    out=w[:, k * HALF:(k + 1) * HALF], in0=ps_of[(t, h)][:], scalar=hsv2col[:, t:t + 1],
-                    in1=hx2b[:, h * HALF:(h + 1) * HALF], op0=ALU.subtract, op1=ALU.subtract)
+                    out=w[:, k * HALF:(k + 1) * HALF], in0=ps_of[(t, h)][:], scalar=norm,
+                    in1=hx2b[:, h * HALF:(h + 1) * HALF], op0=op, op1=ALU.subtract)
 
         def exponent(u):
             width = len(UNITS[u]) * HALF
@@ -291,7 +316,11 @@ def tile_rbf_svm_kernel(tc, X, SV, DC, IC, gamma, out):
         for u in range(2, N_U + 2):
             q = u - 1
             if u < N_U:
-                distances(u)
+                distances(u, FIRST)
+            if by_gram(q + 1):
+                diagonal(q + 1)
+            if u < N_U:
+                distances(u, REST)
             if q + 2 < N_PAIR:
                 squares(q + 2)
             if q + 3 < N_PAIR and not copy_on_vector(q + 3):
@@ -310,6 +339,8 @@ def tile_rbf_svm_kernel(tc, X, SV, DC, IC, gamma, out):
             add_up(u - 2, REST)
             if q + 4 < N_PAIR:
                 in_transposes(q + 4)
+            if by_gram(q + 2):
+                gram(q + 2)
             if u + 1 < N_U:
                 cross(u + 1, REST)
             if q % 2 == 0 and 5 <= q // 2 + 4 < N_MB:

@@ -31,11 +31,17 @@ UNITS = ([[(0, 0), (1, 0)], [(0, 1), (1, 1)]]
          + [[(t, h) for t in (2 * q, 2 * q + 1) for h in range(N_HALF)] for q in range(1, N_PAIR - 1)]
          + [[(N_SVT - 2, 0), (N_SVT - 2, 1)], [(N_SVT - 1, 0)], [(N_SVT - 1, 1)]])
 N_U = len(UNITS)
+N_WORK = 6
+SPARE = 2
 FIRST, REST = slice(0, 2), slice(2, None)
 
 
 def by_gram(q):
     return 4 <= q < N_PAIR - 1 and q % 2 == 0
+
+
+def on_gpsimd(u):
+    return by_gram(u)
 
 FLOPS = 2 * N_ROWS * M_ROWS * D
 
@@ -51,7 +57,6 @@ def tile_rbf_svm_kernel(tc, X, SV, DC, IC, gamma, out):
         keep = ctx.enter_context(tc.tile_pool(name="keep", bufs=1))
         svload = ctx.enter_context(tc.tile_pool(name="svload", bufs=6))
         stage = ctx.enter_context(tc.tile_pool(name="stage", bufs=4))
-        work = ctx.enter_context(tc.tile_pool(name="work", bufs=5))
         junkp = ctx.enter_context(tc.tile_pool(name="junkp", bufs=2))
         ps_mm = ctx.enter_context(tc.psum_pool(name="ps_mm", bufs=4))
         ps_t = ctx.enter_context(tc.psum_pool(name="ps_t", bufs=2))
@@ -110,6 +115,11 @@ def tile_rbf_svm_kernel(tc, X, SV, DC, IC, gamma, out):
         minus_hsv2 = keep.tile([P, N_PAIR], F32)
         dccol = keep.tile([P, N_SVT], F32)
         g2 = const.tile([P, 1], F32)
+        w_buf = []
+        for k in range(N_WORK):
+            buf = keep.tile([P, 2 * N_ROWS + SPARE], F32, name="w%d" % k)
+            nc.gpsimd.memset(buf[:, 2 * N_ROWS:], 0.0)
+            w_buf.append(buf)
         ic_f = const.tile([P, 1], F32)
 
         xq = keep.tile([P, N_ROWS], U32, align_bytes=64)
@@ -236,8 +246,7 @@ def tile_rbf_svm_kernel(tc, X, SV, DC, IC, gamma, out):
                 )
 
         def distances(u, part=slice(None)):
-            if u not in w_of:
-                w_of[u] = work.tile([P, 2 * N_ROWS], F32, name="w")
+            w_of[u] = w_buf[u % N_WORK]
             w = w_of[u]
             for k, (t, h) in list(enumerate(UNITS[u]))[part]:
                 if t % 2 == 0 and by_gram(t // 2):
@@ -246,25 +255,41 @@ def tile_rbf_svm_kernel(tc, X, SV, DC, IC, gamma, out):
                     norm, op = hsv2col[:, t:t + 1], ALU.subtract
                 nc.vector.scalar_tensor_tensor(
                     out=w[:, k * HALF:(k + 1) * HALF], in0=ps_of[(t, h)][:], scalar=norm,
-                    in1=hx2b[:, h * HALF:(h + 1) * HALF], op0=op, op1=ALU.subtract)
+                    in1=hx2b[:, h * HALF:(h + 1) * HALF], op0=op,
+                    op1=ALU.min if k == 0 and on_gpsimd(u) else ALU.subtract)
+                if k == 0 and on_gpsimd(u):
+                    nc.gpsimd.tensor_tensor(out=w[:, :HALF], in0=w[:, :HALF], in1=hx2b[:, :HALF],
+                                            op=ALU.subtract)
 
         def exponent(u):
             width = len(UNITS[u]) * HALF
             nc.scalar.activation(out=w_of[u][:, :width], in_=w_of[u][:, :width], func=ACT.Exp,
                                  scale=g2[:, 0:1])
 
-        def weigh(u):
+        def weigh_columns(u, a, b, t):
             w = w_of[u]
+            nc.vector.tensor_scalar(out=w[:, a:b], in0=w[:, a:b], scalar1=1.0, scalar2=dccol[:, t:t + 1],
+                                    op0=ALU.min, op1=ALU.mult)
+
+        def weigh(u):
             k = 0
             while k < len(UNITS[u]):
                 t = UNITS[u][k][0]
                 e = k + 1
                 while e < len(UNITS[u]) and UNITS[u][e][0] == t:
                     e += 1
-                nc.vector.tensor_scalar(
-                    out=w[:, k * HALF:e * HALF], in0=w[:, k * HALF:e * HALF],
-                    scalar1=1.0, scalar2=dccol[:, t:t + 1], op0=ALU.min, op1=ALU.mult)
+                weigh_columns(u, k * HALF, e * HALF, t)
                 k = e
+
+        def weigh_tile_rest(u):
+            weigh_columns(u, HALF, N_ROWS, UNITS[u][0][0])
+
+        def weigh_with_gpsimd(u):
+            w = w_of[u]
+            weigh_columns(u, N_ROWS, 2 * N_ROWS + SPARE, UNITS[u][2][0])
+            t = UNITS[u][0][0]
+            nc.gpsimd.tensor_scalar(out=w[:, :HALF], in0=w[:, :HALF], scalar1=dccol[:, t:t + 1],
+                                    scalar2=w[:, 2 * N_ROWS:2 * N_ROWS + 1], op0=ALU.mult, op1=ALU.add)
 
         def add_up(u, part=slice(None)):
             w = w_of[u]
@@ -313,7 +338,7 @@ def tile_rbf_svm_kernel(tc, X, SV, DC, IC, gamma, out):
         in_transposes(4)
         load_sv(4)
 
-        for u in range(2, N_U + 2):
+        for u in range(2, N_U + 3):
             q = u - 1
             if u < N_U:
                 distances(u, FIRST)
@@ -328,15 +353,22 @@ def tile_rbf_svm_kernel(tc, X, SV, DC, IC, gamma, out):
             if u < N_U:
                 exponent(u)
             if u - 1 < N_U:
-                weigh(u - 1)
+                if on_gpsimd(u - 1):
+                    weigh_tile_rest(u - 1)
+                else:
+                    weigh(u - 1)
             if q + 2 < N_PAIR:
                 quantise(q + 2)
+            if on_gpsimd(u - 1):
+                weigh_with_gpsimd(u - 1)
             if q + 3 < N_PAIR and copy_on_vector(q + 3):
                 copy_out(q + 3)
-            add_up(u - 2, FIRST)
+            if u >= 3:
+                add_up(u - 3, FIRST)
             if u + 1 < N_U:
                 cross(u + 1, FIRST)
-            add_up(u - 2, REST)
+            if u >= 3:
+                add_up(u - 3, REST)
             if q + 4 < N_PAIR:
                 in_transposes(q + 4)
             if by_gram(q + 2):

@@ -208,13 +208,20 @@ def tile_rbf_svm_kernel(tc, X, SV, DC, IC, gamma, out):
                            hsv2col[:, 2 * q + jj:2 * q + jj + 1], math.sqrt(0.5))
 
         gram_of = {}
+        planes_of = {}
+
+        def spread_planes(q, zero):
+            planes = stage.tile([P, 4, P], BF16, name="planes")
+            planes_of[q] = planes
+            nc.gpsimd.tensor_scalar(out=planes[:],
+                                    in0=grouped_of[q][:, 0:4 * P].rearrange("p (r e) -> p e r", e=4),
+                                    scalar1=1.0, scalar2=zero, op0=ALU.mult, op1=ALU.add)
 
         def gram(q):
             g = ps_mm.tile([P, HALF], F32, name="ps")
             gram_of[q] = g
-            rows = grouped_of[q][:].rearrange("p (r e) -> p r e", e=4)
             for e in range(4):
-                side = rows[:, 0:P, e]
+                side = planes_of[q][:, e, :]
                 nc.tensor.matmul(out=g[:, 0:P], lhsT=side, rhs=side, start=(e == 0), stop=(e == 3))
 
         def diagonal(q):
@@ -281,15 +288,20 @@ def tile_rbf_svm_kernel(tc, X, SV, DC, IC, gamma, out):
                 weigh_columns(u, k * HALF, e * HALF, t)
                 k = e
 
-        def weigh_tile_rest(u):
-            weigh_columns(u, HALF, N_ROWS, UNITS[u][0][0])
+        def zero_of(u):
+            return w_of[u][:, 2 * N_ROWS:2 * N_ROWS + 1]
 
-        def weigh_with_gpsimd(u):
-            w = w_of[u]
+        def weigh_first_tile(u):
+            weigh_columns(u, HALF if on_gpsimd(u) else 0, N_ROWS, UNITS[u][0][0])
+
+        def weigh_second_tile(u):
             weigh_columns(u, N_ROWS, 2 * N_ROWS + SPARE, UNITS[u][2][0])
+
+        def weigh_on_gpsimd(u):
+            w = w_of[u]
             t = UNITS[u][0][0]
             nc.gpsimd.tensor_scalar(out=w[:, :HALF], in0=w[:, :HALF], scalar1=dccol[:, t:t + 1],
-                                    scalar2=w[:, 2 * N_ROWS:2 * N_ROWS + 1], op0=ALU.mult, op1=ALU.add)
+                                    scalar2=zero_of(u), op0=ALU.mult, op1=ALU.add)
 
         def add_up(u, part=slice(None)):
             w = w_of[u]
@@ -352,15 +364,19 @@ def tile_rbf_svm_kernel(tc, X, SV, DC, IC, gamma, out):
                 copy_out(q + 3)
             if u < N_U:
                 exponent(u)
-            if u - 1 < N_U:
-                if on_gpsimd(u - 1):
-                    weigh_tile_rest(u - 1)
-                else:
-                    weigh(u - 1)
+            whole_pair = u - 1 < N_U and len(UNITS[u - 1]) == 2 * N_HALF
+            if whole_pair:
+                weigh_first_tile(u - 1)
+            elif u - 1 < N_U:
+                weigh(u - 1)
             if q + 2 < N_PAIR:
                 quantise(q + 2)
+            if whole_pair:
+                weigh_second_tile(u - 1)
             if on_gpsimd(u - 1):
-                weigh_with_gpsimd(u - 1)
+                weigh_on_gpsimd(u - 1)
+            if by_gram(q + 3):
+                spread_planes(q + 3, zero_of(u - 1))
             if q + 3 < N_PAIR and copy_on_vector(q + 3):
                 copy_out(q + 3)
             if u >= 3:

import math
from contextlib import ExitStack

import concourse.mybir as mybir
from concourse.masks import make_identity

F32 = mybir.dt.float32
BF16 = mybir.dt.bfloat16
U32 = mybir.dt.uint32
U8 = mybir.dt.uint8
FP8X4 = mybir.dt.float8_e4m3fn_x4
ALU = mybir.AluOpType
ACT = mybir.ActivationFunctionType
AX = mybir.AxisListType

P = 128
N_ROWS = 1024
M_ROWS = 8192
D = 512
WORDS = D // 2
NB = N_ROWS // P
HALF = 512
N_HALF = N_ROWS // HALF
JB = HALF // P
MB_COLS = 512
N_MB = M_ROWS // MB_COLS
TILES_PER_MB = MB_COLS // P
N_SVT = M_ROWS // P
N_PAIR = N_SVT // 2
UNITS = ([[(0, 0), (1, 0)], [(0, 1), (1, 1)]]
         + [[(t, h) for t in (2 * q, 2 * q + 1) for h in range(N_HALF)] for q in range(1, N_PAIR - 1)]
         + [[(N_SVT - 2, 0), (N_SVT - 2, 1)], [(N_SVT - 1, 0)], [(N_SVT - 1, 1)]])
N_U = len(UNITS)
N_WORK = 6
SPARE = 2
FIRST, REST = slice(0, 2), slice(2, None)


def by_gram(q):
    return 4 <= q < N_PAIR - 1 and q % 2 == 0


def on_gpsimd(u):
    return by_gram(u)

FLOPS = 2 * N_ROWS * M_ROWS * D


def copy_on_vector(q):
    return q < 2


def tile_rbf_svm_kernel(tc, X, SV, DC, IC, gamma, out):
    nc = tc.nc
    with ExitStack() as ctx:
        const = ctx.enter_context(tc.tile_pool(name="const", bufs=1))
        keep = ctx.enter_context(tc.tile_pool(name="keep", bufs=1))
        svload = ctx.enter_context(tc.tile_pool(name="svload", bufs=6))
        stage = ctx.enter_context(tc.tile_pool(name="stage", bufs=4))
        junkp = ctx.enter_context(tc.tile_pool(name="junkp", bufs=2))
        ps_mm = ctx.enter_context(tc.psum_pool(name="ps_mm", bufs=4))
        ps_t = ctx.enter_context(tc.psum_pool(name="ps_t", bufs=2))
        ps_r = ctx.enter_context(tc.psum_pool(name="ps_r", bufs=1))
        ctx.enter_context(tc.manual_schedule())

        sv_nat = {}

        def load_sv(mb, first=0, tiles=TILES_PER_MB):
            if first == 0:
                sv_nat[mb] = svload.tile([P, TILES_PER_MB * D], BF16, name="sv_nat")
            r0 = mb * MB_COLS + first * P
            nc.sync.dma_start(
                out=sv_nat[mb][:, first * D:(first + tiles) * D].rearrange("p (j d) -> p j d", j=tiles),
                in_=SV[r0:r0 + tiles * P, :].rearrange("(j p) d -> p j d", p=P),
            )

        x_view = X.rearrange("(p j) d -> p j d", j=NB)
        x_nat = [keep.tile([P, JB * D], BF16, name="x_nat%d" % h) for h in range(N_HALF)]

        def load_x(h):
            for a in range(2):
                nc.sync.dma_start(
                    out=x_nat[h][:, a * 2 * D:(a + 1) * 2 * D].rearrange("p (j d) -> p j d", j=2),
                    in_=x_view[:, h * JB + 2 * a:h * JB + 2 * a + 2, :])

        load_x(0)
        load_sv(0, 0, 2)
        load_x(1)
        load_sv(0, 2, 2)
        load_sv(1)
        load_sv(2)
        load_sv(3)

        dc_rows = const.tile([P, P], BF16)
        nc.vector.memset(dc_rows[:], 0.0)
        warm = const.tile([P, 1], F32)
        nc.vector.memset(warm[:], 0.0)
        g_bf = const.tile([P, 1], BF16)
        nc.scalar.dma_start(out=g_bf[:], in_=gamma.partition_broadcast(P))
        ic_bf = const.tile([P, 1], BF16)
        nc.scalar.dma_start(out=ic_bf[:], in_=IC.partition_broadcast(P))
        nc.scalar.dma_start(out=dc_rows[0:N_SVT, :], in_=DC.rearrange("o (t p) -> (o t) p", p=P))
        nc.scalar.activation(out=warm[:], in_=warm[:], func=ACT.Exp)

        ident = const.tile([P, P], F32)
        make_identity(nc, ident[:])
        ident_bf = const.tile([P, P], BF16)
        nc.vector.tensor_copy(out=ident_bf[:], in_=ident[:])
        half_ident = const.tile([P, P], F32)
        nc.vector.tensor_scalar(out=half_ident[:], in0=ident[:], scalar1=0.5, scalar2=None, op0=ALU.mult)

        x2col = keep.tile([P, NB], F32)
        hx2b = keep.tile([P, N_ROWS], F32)
        hsv2col = keep.tile([P, N_SVT], F32)
        minus_hsv2 = keep.tile([P, N_PAIR], F32)
        dccol = keep.tile([P, N_SVT], F32)
        g2 = const.tile([P, 1], F32)
        w_buf = []
        for k in range(N_WORK):
            buf = keep.tile([P, 2 * N_ROWS + SPARE], F32, name="w%d" % k)
            nc.gpsimd.memset(buf[:, 2 * N_ROWS:], 0.0)
            w_buf.append(buf)
        ic_f = const.tile([P, 1], F32)

        xq = keep.tile([P, N_ROWS], U32, align_bytes=64)
        xs = keep.tile([P, N_ROWS], U8, align_bytes=64)
        svq = keep.tile([P, M_ROWS], U32, align_bytes=64)
        svs = keep.tile([P, M_ROWS], U8, align_bytes=64)
        acc = [ps_r.tile([P, JB, P], F32, name="acc%d" % h) for h in range(N_HALF)]

        def transpose_pair(src_f32, first_tile):
            xt = ps_t.tile([P, 4, P], F32, name="xt")
            for jj in range(2):
                for u in range(2):
                    c0 = (first_tile + jj) * WORDS + u * P
                    nc.tensor.transpose(xt[:, 2 * jj + u, :], src_f32[:, c0:c0 + P], ident[:])
            return xt

        def copy_pair(xt, dst_f32, on_vector):
            dst = dst_f32.rearrange("p (j r u) -> p j r u", j=2, u=2)
            src = xt[:].rearrange("p (j u) r -> p j r u", j=2)
            if on_vector:
                nc.vector.tensor_copy(out=dst, in_=src)
            else:
                nc.scalar.copy(out=dst, in_=src)

        def square_sum(src, col, scale):
            junk = junkp.tile([P, D], BF16, name="junk")
            nc.scalar.activation(out=junk[:], in_=src, func=ACT.Square, scale=scale, accum_out=col)

        gx = keep.tile([P, N_ROWS * 4], BF16, align_bytes=64)
        gx_f32 = gx[:].bitcast(F32)

        def x_squares(h):
            for jj in range(JB):
                j = h * JB + jj
                square_sum(x_nat[h][:, jj * D:(jj + 1) * D], x2col[:, j:j + 1], 1.0)

        xt_x = {}

        def x_transposes(h):
            for pr in range(JB // 2):
                xt_x[(h, pr)] = transpose_pair(x_nat[h][:].bitcast(F32), 2 * pr)

        def x_quantise(h):
            for pr in range(JB // 2):
                k = h * (JB // 2) + pr
                copy_pair(xt_x[(h, pr)], gx_f32[:, k * 512:(k + 1) * 512], True)
            nc.vector.quantize_mx(out=xq[:, h * HALF:(h + 1) * HALF].bitcast(FP8X4),
                                  scales=xs[:, h * HALF:(h + 1) * HALF],
                                  in_=gx[:, h * HALF * 4:(h + 1) * HALF * 4])

        bc_of = {}

        def spread_x_norms(h):
            bc_of[h] = ps_mm.tile([P, HALF], F32, name="ps")
            for jj in range(JB):
                j = h * JB + jj
                nc.tensor.matmul(out=bc_of[h][:, jj * P:(jj + 1) * P],
                                 lhsT=x2col[:, j:j + 1].to_broadcast([P, P]),
                                 rhs=half_ident[:], start=True, stop=True)

        def keep_x_norms(h):
            nc.vector.tensor_copy(out=hx2b[:, h * HALF:(h + 1) * HALF], in_=bc_of[h][:])

        def dc_to_columns():
            dct = ps_t.tile([P, P], BF16, name="xt")
            nc.tensor.transpose(dct[:], dc_rows[:], ident_bf[:])
            nc.vector.tensor_copy(out=dccol[:], in_=dct[:, 0:N_SVT])
            nc.vector.tensor_copy(out=ic_f[:], in_=ic_bf[:])

        xt_of = {}
        grouped_of = {}
        ps_of = {}
        w_of = {}

        def pair_src(q):
            return sv_nat[q // 2], (q % 2) * 2

        def in_transposes(q):
            t, first = pair_src(q)
            xt_of[q] = transpose_pair(t[:].bitcast(F32), first)

        def squares(q):
            t, first = pair_src(q)
            for jj in range(1 if by_gram(q) else 0, 2):
                square_sum(t[:, (first + jj) * D:(first + jj + 1) * D],
                           hsv2col[:, 2 * q + jj:2 * q + jj + 1], math.sqrt(0.5))

        gram_of = {}
        planes_of = {}

        def spread_planes(q, zero):
            planes = stage.tile([P, 4, P], BF16, name="planes")
            planes_of[q] = planes
            nc.gpsimd.tensor_scalar(out=planes[:],
                                    in0=grouped_of[q][:, 0:4 * P].rearrange("p (r e) -> p e r", e=4),
                                    scalar1=1.0, scalar2=zero, op0=ALU.mult, op1=ALU.add)

        def gram(q):
            g = ps_mm.tile([P, HALF], F32, name="ps")
            gram_of[q] = g
            for e in range(4):
                side = planes_of[q][:, e, :]
                nc.tensor.matmul(out=g[:, 0:P], lhsT=side, rhs=side, start=(e == 0), stop=(e == 3))

        def diagonal(q):
            junk = junkp.tile([P, P], F32, name="junk_g")
            nc.vector.scalar_tensor_tensor(out=junk[:], in0=gram_of[q][:, 0:P], scalar=-0.5, in1=ident[:],
                                           op0=ALU.mult, op1=ALU.mult,
                                           accum_out=minus_hsv2[:, q:q + 1])

        def copy_out(q):
            grouped = stage.tile([P, 2 * P * 4], BF16, align_bytes=64, name="grouped")
            grouped_of[q] = grouped
            copy_pair(xt_of[q], grouped[:].bitcast(F32), copy_on_vector(q))

        def quantise(q):
            cols = slice(q * 2 * P, (q + 1) * 2 * P)
            nc.vector.quantize_mx(out=svq[:, cols].bitcast(FP8X4), scales=svs[:, cols], in_=grouped_of[q][:])

        def cross(u, part=slice(None)):
            for t, h in UNITS[u][part]:
                ps = ps_mm.tile([P, HALF], F32, name="ps")
                ps_of[(t, h)] = ps
                nc.tensor.matmul_mx(
                    out=ps[:],
                    lhsT=svq[:, t * P:(t + 1) * P].bitcast(FP8X4),
                    lhsT_scale=svs[:, t * P:(t + 1) * P],
                    rhs=xq[:, h * HALF:(h + 1) * HALF].bitcast(FP8X4),
                    rhs_scale=xs[:, h * HALF:(h + 1) * HALF],
                    start=True, stop=True,
                )

        def distances(u, part=slice(None)):
            w_of[u] = w_buf[u % N_WORK]
            w = w_of[u]
            for k, (t, h) in list(enumerate(UNITS[u]))[part]:
                if t % 2 == 0 and by_gram(t // 2):
                    norm, op = minus_hsv2[:, t // 2:t // 2 + 1], ALU.add
                else:
                    norm, op = hsv2col[:, t:t + 1], ALU.subtract
                nc.vector.scalar_tensor_tensor(
                    out=w[:, k * HALF:(k + 1) * HALF], in0=ps_of[(t, h)][:], scalar=norm,
                    in1=hx2b[:, h * HALF:(h + 1) * HALF], op0=op,
                    op1=ALU.min if k == 0 and on_gpsimd(u) else ALU.subtract)
                if k == 0 and on_gpsimd(u):
                    nc.gpsimd.tensor_tensor(out=w[:, :HALF], in0=w[:, :HALF], in1=hx2b[:, :HALF],
                                            op=ALU.subtract)

        def exponent(u):
            width = len(UNITS[u]) * HALF
            nc.scalar.activation(out=w_of[u][:, :width], in_=w_of[u][:, :width], func=ACT.Exp,
                                 scale=g2[:, 0:1])

        def weigh_columns(u, a, b, t):
            w = w_of[u]
            nc.vector.tensor_scalar(out=w[:, a:b], in0=w[:, a:b], scalar1=1.0, scalar2=dccol[:, t:t + 1],
                                    op0=ALU.min, op1=ALU.mult)

        def weigh(u):
            k = 0
            while k < len(UNITS[u]):
                t = UNITS[u][k][0]
                e = k + 1
                while e < len(UNITS[u]) and UNITS[u][e][0] == t:
                    e += 1
                weigh_columns(u, k * HALF, e * HALF, t)
                k = e

        def zero_of(u):
            return w_of[u][:, 2 * N_ROWS:2 * N_ROWS + 1]

        def weigh_first_tile(u):
            weigh_columns(u, HALF if on_gpsimd(u) else 0, N_ROWS, UNITS[u][0][0])

        def weigh_second_tile(u):
            weigh_columns(u, N_ROWS, 2 * N_ROWS + SPARE, UNITS[u][2][0])

        def weigh_on_gpsimd(u):
            w = w_of[u]
            t = UNITS[u][0][0]
            nc.gpsimd.tensor_scalar(out=w[:, :HALF], in0=w[:, :HALF], scalar1=dccol[:, t:t + 1],
                                    scalar2=zero_of(u), op0=ALU.mult, op1=ALU.add)

        def add_up(u, part=slice(None)):
            w = w_of[u]
            for k, (t, h) in list(enumerate(UNITS[u]))[part]:
                for jj in range(JB):
                    o = k * HALF + jj * P
                    nc.tensor.matmul(out=acc[h][:, jj, :], lhsT=w[:, o:o + P],
                                     rhs=ident[:], is_transpose=True,
                                     start=(t == 0 and jj == 0),
                                     stop=(t == N_SVT - 1 and jj == JB - 1))

        x_squares(0)
        x_transposes(0)
        x_quantise(0)
        nc.vector.tensor_scalar(out=g2[:], in0=g_bf[:], scalar1=2.0, scalar2=None, op0=ALU.mult)
        in_transposes(0)
        squares(0)
        spread_x_norms(0)
        copy_out(0)
        x_transposes(1)
        quantise(0)
        keep_x_norms(0)
        cross(0)
        x_squares(1)
        distances(0)
        spread_x_norms(1)
        x_quantise(1)
        in_transposes(1)
        exponent(0)
        copy_out(1)
        dc_to_columns()
        squares(1)
        keep_x_norms(1)
        in_transposes(2)
        quantise(1)
        copy_out(2)
        cross(1)
        distances(1)
        exponent(1)
        weigh(0)
        in_transposes(3)
        squares(2)
        cross(2)
        quantise(2)
        copy_out(3)
        in_transposes(4)
        load_sv(4)

        for u in range(2, N_U + 3):
            q = u - 1
            if u < N_U:
                distances(u, FIRST)
            if by_gram(q + 1):
                diagonal(q + 1)
            if u < N_U:
                distances(u, REST)
            if q + 2 < N_PAIR:
                squares(q + 2)
            if q + 3 < N_PAIR and not copy_on_vector(q + 3):
                copy_out(q + 3)
            if u < N_U:
                exponent(u)
            whole_pair = u - 1 < N_U and len(UNITS[u - 1]) == 2 * N_HALF
            if whole_pair:
                weigh_first_tile(u - 1)
            elif u - 1 < N_U:
                weigh(u - 1)
            if q + 2 < N_PAIR:
                quantise(q + 2)
            if whole_pair:
                weigh_second_tile(u - 1)
            if on_gpsimd(u - 1):
                weigh_on_gpsimd(u - 1)
            if by_gram(q + 3):
                spread_planes(q + 3, zero_of(u - 1))
            if q + 3 < N_PAIR and copy_on_vector(q + 3):
                copy_out(q + 3)
            if u >= 3:
                add_up(u - 3, FIRST)
            if u + 1 < N_U:
                cross(u + 1, FIRST)
            if u >= 3:
                add_up(u - 3, REST)
            if q + 4 < N_PAIR:
                in_transposes(q + 4)
            if by_gram(q + 2):
                gram(q + 2)
            if u + 1 < N_U:
                cross(u + 1, REST)
            if q % 2 == 0 and 5 <= q // 2 + 4 < N_MB:
                load_sv(q // 2 + 4)

        res = const.tile([P, NB], F32)
        for h in range(N_HALF):
            nc.vector.tensor_reduce(out=res[:, h * JB:(h + 1) * JB], in_=acc[h][:], axis=AX.X, op=ALU.add)
        res2 = const.tile([P, NB], F32)
        nc.vector.tensor_scalar(out=res2[:], in0=res[:], scalar1=ic_f[:, 0:1], scalar2=None, op0=ALU.add)
        nc.sync.dma_start(out=out.rearrange("(p j) -> p j", j=NB), in_=res2[:])
